import numpy as np
import ml_dtypes


def mxq(x, axis, fmt="e4m3"):
    dtype, down = {"e4m3": (ml_dtypes.float8_e4m3fn, 7), "e5m2": (ml_dtypes.float8_e5m2, 14)}[fmt]
    v = np.moveaxis(np.asarray(x, np.float32).astype(ml_dtypes.bfloat16).astype(np.float64), axis, -1)
    blocks = v.reshape(v.shape[:-1] + (-1, 32))
    amax = np.abs(blocks).max(-1, keepdims=True)
    byte = np.maximum(np.where(amax > 0, np.frexp(amax)[1] - 1 + 127, 0) - down, 1)
    scale = np.exp2(byte - 127.0)
    codes = (blocks / scale).astype(np.float32).astype(dtype).astype(np.float64)
    return np.moveaxis((codes * scale).reshape(v.shape), -1, axis)


WIDE = False


def mx_kscale(k):
    if not WIDE:
        return np.ones(k)
    levels = np.array([30, -30])
    if k % 512:
        return np.exp2(np.random.permutation(np.resize(levels, k // 32))).repeat(32)
    a = np.empty((k // 512, 16))
    for p in range(k // 512):
        a[p, :8] = np.random.permutation(np.resize(levels, 8))
        for g in range(8):
            far = levels[np.abs(levels - a[p, g]) >= 10]
            a[p, g + 8] = far[np.random.randint(len(far))]
    return np.exp2(a.ravel()).repeat(32)


BF16 = ml_dtypes.bfloat16


def bf(x):
    return np.asarray(x, np.float32).astype(BF16)


def f64(x):
    return np.asarray(x).astype(np.float64)


B, S, HID, H, DH = 1, 512, 2048, 16, 128
INNER = H * DH
HALF = DH // 2
ROPE_BASE = 10000.0


def heads(y):
    return y.reshape(B, S, H, DH).transpose(0, 2, 1, 3)


def apply_rope(x):
    inv_freq = 1.0 / ROPE_BASE ** (np.arange(0, DH, 2) / DH)
    freqs = np.arange(S)[:, None] * inv_freq[None, :]
    cos = np.concatenate([np.cos(freqs)] * 2, -1)
    sin = np.concatenate([np.sin(freqs)] * 2, -1)
    x1, x2 = x[..., :HALF], x[..., HALF:]
    rotated = np.concatenate([-x2, x1], -1)
    return x * cos[None, None] + rotated * sin[None, None]


def setup_inputs():
    s = mx_kscale(HID)
    return {"hidden_states": bf(np.random.standard_normal((B, S, HID)) * s),
            "Wq": bf(np.random.standard_normal((INNER, HID)) * 1.2 / np.sqrt(HID) / s),
            "bq": bf(np.random.standard_normal(INNER) * 0.3),
            "Wk": bf(np.random.standard_normal((INNER, HID)) * 1.2 / np.sqrt(HID) / s),
            "bk": bf(np.random.standard_normal(INNER) * 0.3)}


def reference(hidden_states, Wq, bq, Wk, bk):
    xq = mxq(f64(hidden_states), 2, "e5m2")
    q = heads((xq @ mxq(f64(Wq).T, 0, "e5m2")) + f64(bq))
    k = heads((xq @ mxq(f64(Wk).T, 0, "e5m2")) + f64(bk))
    return apply_rope(q), apply_rope(k)

@@ -1,0 +1,327 @@
+import math
+from contextlib import ExitStack
+
+import concourse.mybir as mybir
+from concourse.masks import make_identity
+
+F32 = mybir.dt.float32
+BF16 = mybir.dt.bfloat16
+U32 = mybir.dt.uint32
+U8 = mybir.dt.uint8
+I32 = mybir.dt.int32
+FP8X4 = mybir.dt.float8_e5m2_x4
+ALU = mybir.AluOpType
+ACT = mybir.ActivationFunctionType
+
+P = 128
+S = 512
+HID = 2048
+DH = 128
+HALF = 64
+N_TOK = 4
+N_PASS = 4
+N_GRP = 8
+GRP = 512
+ROPE_BASE = 10000.0
+FLOPS = 2 * S * HID * 2 * HID
+
+
+def tile_densemha_pa_kernel(tc, hidden_states, Wq, bq, Wk, bk, out_0, out_1):
+    nc = tc.nc
+    with ExitStack() as ctx:
+        const = ctx.enter_context(tc.tile_pool(name="const", bufs=1))
+        xraw_pool = ctx.enter_context(tc.tile_pool(name="xraw", bufs=4))
+        raw_pool = ctx.enter_context(tc.tile_pool(name="raw", bufs=6))
+        grp_pool = ctx.enter_context(tc.tile_pool(name="grp", bufs=6))
+        wcode_pool = ctx.enter_context(tc.tile_pool(name="wcode", bufs=3))
+        ep_pool = ctx.enter_context(tc.tile_pool(name="ep", bufs=2))
+        tp_pool = ctx.enter_context(tc.psum_pool(name="tp", bufs=4))
+        acc_pool = ctx.enter_context(tc.psum_pool(name="acc", bufs=4))
+
+        xraw = {}
+        wraw = {}
+
+        def load_x(a):
+            t = xraw_pool.tile([P, HID], BF16, name="xr")
+            nc.sync.dma_start(out=t[:], in_=hidden_states[0, a * P:(a + 1) * P, :])
+            xraw[a] = t
+
+        def load_w(n):
+            w = Wq if n < 4 else Wk
+            r0 = (n % 4) * GRP
+            for h in range(2):
+                t = raw_pool.tile([P, 4, HID // 2], BF16, name="wr")
+                nc.sync.dma_start(
+                    out=t[:],
+                    in_=w[r0:r0 + GRP, h * 1024:(h + 1) * 1024].rearrange("(t p) k -> p t k", p=P),
+                )
+                wraw[(n, h)] = t
+
+        brow = const.tile([P, GRP], BF16, name="brow")
+        nc.vector.memset(brow[:], 0.0)
+        nc.scalar.dma_start(out=brow[0:4, :], in_=bq.rearrange("(j n) -> j n", n=GRP))
+        nc.scalar.dma_start(out=brow[4:8, :], in_=bk.rearrange("(j n) -> j n", n=GRP))
+
+        load_x(0)
+        load_x(1)
+        load_w(0)
+        load_x(2)
+        load_x(3)
+        load_w(1)
+        load_w(2)
+
+        zero_col = const.tile([P, 1], F32, name="zero_col")
+        nc.vector.memset(zero_col[:], 0.0)
+        warm = const.tile([P, 1], F32, name="warm")
+        nc.scalar.activation(out=warm[:], in_=zero_col[:], func=ACT.Sin)
+
+        ident = const.tile([P, P], F32, name="ident")
+        make_identity(nc, ident[:])
+        ident_bf = const.tile([P, P], BF16, name="ident_bf")
+        make_identity(nc, ident_bf[:])
+
+        tpos_i = const.tile([P, N_TOK], I32, name="tpos_i")
+        nc.gpsimd.iota(tpos_i[:], pattern=[[P, N_TOK]], base=0, channel_multiplier=1)
+        tpos = const.tile([P, N_TOK], F32, name="tpos")
+        nc.vector.tensor_copy(out=tpos[:], in_=tpos_i[:])
+        one_col = const.tile([P, 1], F32, name="one_col")
+        nc.vector.memset(one_col[:], 1.0)
+        freq = const.tile([P, HALF], F32, name="freq")
+        for i in range(8):
+            nc.vector.tensor_scalar(
+                out=freq[:, i:i + 1], in0=one_col[:], scalar1=ROPE_BASE ** (-i / 64.0) / (2.0 * math.pi),
+                scalar2=None, op0=ALU.mult,
+            )
+        for j in range(1, 8):
+            nc.vector.tensor_scalar(
+                out=freq[:, 8 * j:8 * j + 8], in0=freq[:, 0:8], scalar1=ROPE_BASE ** (-8 * j / 64.0),
+                scalar2=None, op0=ALU.mult,
+            )
+        NT = N_TOK * HALF
+        turns = const.tile([P, NT], F32, name="turns")
+        for a in range(N_TOK):
+            nc.vector.tensor_scalar(
+                out=turns[:, a * HALF:(a + 1) * HALF], in0=freq[:], scalar1=tpos[:, a:a + 1],
+                scalar2=None, op0=ALU.mult,
+            )
+        whole = const.tile([P, NT], I32, name="whole")
+        nc.vector.tensor_scalar(out=whole[:], in0=turns[:], scalar1=1.0, scalar2=-1.0e-4, op0=ALU.mult, op1=ALU.add)
+        frac = const.tile([P, NT], F32, name="frac")
+        nc.vector.scalar_tensor_tensor(out=frac[:], in0=whole[:], scalar=-1.0, in1=turns[:], op0=ALU.mult, op1=ALU.add)
+        neg_s = const.tile([P, NT], F32, name="neg_s")
+        nc.vector.scalar_tensor_tensor(out=neg_s[:], in0=frac[:], scalar=0.5, in1=frac[:], op0=ALU.is_gt, op1=ALU.subtract)
+        quart = const.tile([P, NT], F32, name="quart")
+        nc.vector.tensor_scalar(out=quart[:], in0=neg_s[:], scalar1=-1.0, scalar2=0.25, op0=ALU.mult, op1=ALU.add)
+        neg_c = const.tile([P, NT], F32, name="neg_c")
+        nc.vector.scalar_tensor_tensor(out=neg_c[:], in0=quart[:], scalar=0.5, in1=quart[:], op0=ALU.is_gt, op1=ALU.subtract)
+
+        cos_t = const.tile([P, N_TOK, 1, DH], F32, name="cos_t")
+        sin_t = const.tile([P, N_TOK, 1, DH], F32, name="sin_t")
+        ns3 = neg_s[:].rearrange("p (a i) -> p a i", a=N_TOK)
+        nc3 = neg_c[:].rearrange("p (a i) -> p a i", a=N_TOK)
+        two_pi = 2.0 * math.pi
+        nc.scalar.activation(out=sin_t[:, :, 0, 0:HALF], in_=ns3, func=ACT.Sin, scale=two_pi)
+        nc.scalar.activation(out=sin_t[:, :, 0, HALF:DH], in_=ns3, func=ACT.Sin, scale=-two_pi)
+        nc.scalar.activation(out=cos_t[:, :, 0, 0:HALF], in_=nc3, func=ACT.Sin, scale=-two_pi)
+        nc.scalar.activation(out=cos_t[:, :, 0, HALF:DH], in_=nc3, func=ACT.Sin, scale=-two_pi)
+
+        bias_sb = const.tile([P, N_GRP, GRP], F32, name="bias_sb")
+
+        def bias_bcast(n):
+            bank = tp_pool.tile([P, GRP], F32, name="bank")
+            nc.tensor.matmul(out=bank[:], lhsT=ident_bf[:, n:n + 1].to_broadcast([P, P]), rhs=brow[:], start=True, stop=True)
+            nc.scalar.copy(out=bias_sb[:, n, :], in_=bank[:])
+
+        def transpose_unit(blocks):
+            grouped = grp_pool.tile([P, 4, P, 4], BF16, name="grouped", align_bytes=64)
+            gw = grouped[:].bitcast(F32)
+            for half in range(2):
+                bank = tp_pool.tile([P, 2, 2, P], F32, name="bank")
+                for s in range(2):
+                    for u in range(2):
+                        nc.tensor.transpose(bank[:, s, u, :], blocks[2 * half + s][:, u::2], ident[:])
+                nc.scalar.copy(out=gw[:, 2 * half:2 * half + 2, :, :], in_=bank[:].rearrange("p s u r -> p s r u"))
+            return grouped
+
+        def quantize(grouped, codes, scales):
+            nc.vector.quantize_mx(out=codes.bitcast(FP8X4), scales=scales, in_=grouped[:].rearrange("p b r j -> p (b r j)"))
+
+        xq = {}
+        xs = {}
+        xg = {}
+
+        def tr_x(a):
+            words = xraw[a][:].bitcast(F32)
+            xg[a] = transpose_unit([words[:, 256 * g:256 * (g + 1)] for g in range(N_PASS)])
+
+        def qz_x(a):
+            xq[a] = const.tile([P, N_PASS * P], U32, name="xq%d" % a, align_bytes=64)
+            xs[a] = const.tile([P, N_PASS * P], U8, name="xs%d" % a, align_bytes=64)
+            quantize(xg[a], xq[a][:], xs[a][:])
+
+        wq = {}
+        ws = {}
+        wg = {}
+
+        def tr_w(n, g):
+            if n >= N_GRP:
+                return
+            if g == 0:
+                bias_bcast(n)
+            words = wraw[(n, g // 2)][:].bitcast(F32)
+            c0 = 256 * (g % 2)
+            wg[(n, g)] = transpose_unit([words[:, t, c0:c0 + 256] for t in range(4)])
+
+        def qz_w(n, g):
+            if n >= N_GRP:
+                return
+            if g == 0:
+                wq[n] = wcode_pool.tile([P, N_PASS, GRP], U32, name="wq", align_bytes=64)
+                ws[n] = wcode_pool.tile([P, N_PASS, GRP], U8, name="ws", align_bytes=64)
+            quantize(wg[(n, g)], wq[n][:, g, :], ws[n][:, g, :])
+
+        acc = {}
+
+        def mm(n, a):
+            if n >= N_GRP:
+                return
+            t = acc_pool.tile([P, GRP], F32, name="acc")
+            acc[(n, a)] = t
+            for g in range(N_PASS):
+                cols = slice(g * P, (g + 1) * P)
+                nc.tensor.matmul_mx(
+                    out=t[:],
+                    lhsT=xq[a][:, cols].bitcast(FP8X4),
+                    lhsT_scale=xs[a][:, cols],
+                    rhs=wq[n][:, g, :].bitcast(FP8X4),
+                    rhs_scale=ws[n][:, g, :],
+                    start=(g == 0),
+                    stop=(g == N_PASS - 1),
+                )
+
+        ys = {}
+        rots = {}
+        ress = {}
+
+        def ep_tiles(n):
+            ys[n] = ep_pool.tile([P, N_TOK, 4, DH], F32, name="y")
+            rots[n] = ep_pool.tile([P, N_TOK, 4, DH], F32, name="rot")
+            ress[n] = ep_pool.tile([P, N_TOK, 4, DH], F32, name="res")
+
+        def add_bias(n, a):
+            nc.vector.tensor_tensor(
+                out=ys[n][:, a, :, :].rearrange("p h f -> p (h f)"), in0=acc[(n, a)][:], in1=bias_sb[:, n, :], op=ALU.add
+            )
+
+        def rope_mul(n, a0, a1):
+            y, rot, res = ys[n], rots[n], ress[n]
+            k = a1 - a0
+            nc.vector.tensor_tensor(
+                out=rot[:, a0:a1, :, 0:HALF], in0=y[:, a0:a1, :, HALF:DH],
+                in1=sin_t[:, a0:a1, :, 0:HALF].to_broadcast([P, k, 4, HALF]), op=ALU.mult,
+            )
+            nc.vector.tensor_tensor(
+                out=rot[:, a0:a1, :, HALF:DH], in0=y[:, a0:a1, :, 0:HALF],
+                in1=sin_t[:, a0:a1, :, HALF:DH].to_broadcast([P, k, 4, HALF]), op=ALU.mult,
+            )
+            nc.vector.tensor_tensor(
+                out=res[:, a0:a1, :, :], in0=y[:, a0:a1, :, :],
+                in1=cos_t[:, a0:a1, :, :].to_broadcast([P, k, 4, DH]), op=ALU.mult,
+            )
+
+        def rope_add(n, a0, a1):
+            rot, res = rots[n], ress[n]
+            nc.vector.tensor_tensor(out=res[:, a0:a1, :, :], in0=res[:, a0:a1, :, :], in1=rot[:, a0:a1, :, :], op=ALU.add)
+            dst = out_0 if n < 4 else out_1
+            h0 = 4 * (n % 4)
+            for a in range(a0, a1):
+                nc.sync.dma_start(
+                    out=dst[0, h0:h0 + 4, a * P:(a + 1) * P, :].rearrange("h p f -> p h f"), in_=res[:, a, :, :]
+                )
+
+        tr_x(0)
+        tr_x(1)
+        tr_w(0, 0)
+        qz_x(0)
+        tr_w(0, 1)
+        qz_x(1)
+        tr_w(0, 2)
+        qz_w(0, 0)
+        tr_w(0, 3)
+        qz_w(0, 1)
+        tr_x(2)
+        qz_w(0, 2)
+        tr_x(3)
+        qz_w(0, 3)
+        qz_x(2)
+        qz_x(3)
+
+        ep_tiles(0)
+        mm(0, 0)
+        mm(0, 1)
+        add_bias(0, 0)
+        mm(0, 2)
+        rope_mul(0, 0, 1)
+        add_bias(0, 1)
+        mm(0, 3)
+        rope_add(0, 0, 1)
+        rope_mul(0, 1, 2)
+        tr_w(1, 0)
+        tr_w(1, 1)
+        add_bias(0, 2)
+        rope_add(0, 1, 2)
+        qz_w(1, 0)
+        rope_mul(0, 2, 3)
+        add_bias(0, 3)
+        tr_w(1, 2)
+        tr_w(1, 3)
+        rope_add(0, 2, 3)
+        qz_w(1, 1)
+        rope_mul(0, 3, 4)
+        qz_w(1, 2)
+        rope_add(0, 3, 4)
+        qz_w(1, 3)
+        load_w(3)
+        tr_w(2, 0)
+        tr_w(2, 1)
+        mm(1, 0)
+        mm(1, 1)
+        qz_w(2, 0)
+        tr_w(2, 2)
+        tr_w(2, 3)
+        qz_w(2, 1)
+        mm(1, 2)
+        mm(1, 3)
+        qz_w(2, 2)
+        qz_w(2, 3)
+
+        for c in range(1, N_GRP):
+            if c + 3 < N_GRP:
+                load_w(c + 3)
+            ep_tiles(c)
+            tr_w(c + 2, 0)
+            tr_w(c + 2, 1)
+            for a in range(N_TOK):
+                add_bias(c, a)
+            qz_w(c + 2, 0)
+            mm(c + 1, 0)
+            mm(c + 1, 1)
+            if c < N_GRP - 1:
+                rope_mul(c, 0, 4)
+                tr_w(c + 2, 2)
+                tr_w(c + 2, 3)
+                qz_w(c + 2, 1)
+                rope_add(c, 0, 4)
+                mm(c + 1, 2)
+                mm(c + 1, 3)
+                qz_w(c + 2, 2)
+                qz_w(c + 2, 3)
+            else:
+                rope_mul(c, 0, 1)
+                rope_mul(c, 1, 2)
+                rope_add(c, 0, 1)
+                rope_mul(c, 2, 3)
+                rope_add(c, 1, 2)
+                rope_mul(c, 3, 4)
+                rope_add(c, 2, 3)
+                rope_add(c, 3, 4)

@@ -22,6 +22,8 @@ N_TOK = 4
 N_PASS = 4
 N_GRP = 8
 GRP = 512
+N_PAIR = 16
+RAW_BUFS = 6
 ROPE_BASE = 10000.0
 FLOPS = 2 * S * HID * 2 * HID
 
@@ -30,45 +32,58 @@ def tile_densemha_pa_kernel(tc, hidden_states, Wq, bq, Wk, bk, out_0, out_1):
     nc = tc.nc
     with ExitStack() as ctx:
         const = ctx.enter_context(tc.tile_pool(name="const", bufs=1))
-        xraw_pool = ctx.enter_context(tc.tile_pool(name="xraw", bufs=4))
-        raw_pool = ctx.enter_context(tc.tile_pool(name="raw", bufs=6))
+        head_pool = ctx.enter_context(tc.tile_pool(name="head", bufs=8))
+        raw_pool = ctx.enter_context(tc.tile_pool(name="raw", bufs=RAW_BUFS))
         grp_pool = ctx.enter_context(tc.tile_pool(name="grp", bufs=6))
         wcode_pool = ctx.enter_context(tc.tile_pool(name="wcode", bufs=3))
-        ep_pool = ctx.enter_context(tc.tile_pool(name="ep", bufs=2))
+        ep_pool = ctx.enter_context(tc.tile_pool(name="ep", bufs=3))
         tp_pool = ctx.enter_context(tc.psum_pool(name="tp", bufs=4))
         acc_pool = ctx.enter_context(tc.psum_pool(name="acc", bufs=4))
 
-        xraw = {}
-        wraw = {}
+        def seq_src(s):
+            if s == 0 or s == 2:
+                return (-1, s // 2)
+            if s == 1 or s == 3:
+                return (0, s // 2)
+            return ((s - 2) // 2, s % 2)
 
-        def load_x(a):
-            t = xraw_pool.tile([P, HID], BF16, name="xr")
-            nc.sync.dma_start(out=t[:], in_=hidden_states[0, a * P:(a + 1) * P, :])
-            xraw[a] = t
+        N_SEQ = 2 * N_GRP + 2
+        raw = {}
 
-        def load_w(n):
-            w = Wq if n < 4 else Wk
-            r0 = (n % 4) * GRP
-            for h in range(2):
+        def load(s):
+            if s >= N_SEQ:
+                return
+            n, h = seq_src(s)
+            if n < 0:
+                rows = hidden_states[0, :, h * 1024:(h + 1) * 1024]
+            else:
+                w = Wq if n < 4 else Wk
+                r0 = (n % 4) * GRP
+                rows = w[r0:r0 + GRP, h * 1024:(h + 1) * 1024]
+            view = rows.rearrange("(t p) k -> p t k", p=P)
+            if s < 4:
+                for e in range(2):
+                    t = head_pool.tile([P, 4, GRP], BF16, name="wh")
+                    nc.sync.dma_start(out=t[:], in_=view[:, :, e * GRP:(e + 1) * GRP])
+                    raw[(s, e)] = (t, 0)
+            else:
                 t = raw_pool.tile([P, 4, HID // 2], BF16, name="wr")
-                nc.sync.dma_start(
-                    out=t[:],
-                    in_=w[r0:r0 + GRP, h * 1024:(h + 1) * 1024].rearrange("(t p) k -> p t k", p=P),
+                nc.sync.dma_start(out=t[:], in_=view)
+                raw[(s, 0)] = (t, 0)
+                raw[(s, 1)] = (t, 256)
+
+        zrows = const.tile([P, P], BF16, name="zrows")
+        nc.vector.memset(zrows[:], 0.0)
+        for v, b in enumerate((bq, bk)):
+            bv = b.rearrange("(m x y r) -> x y m r", x=2, y=2, r=HALF)
+            for y in range(2):
+                r0 = v * 16 + y * 8
+                nc.scalar.dma_start(
+                    out=zrows[r0:r0 + 8, :].rearrange("m (x r) -> m x r", x=2), in_=bv[:, y].rearrange("x m r -> m x r")
                 )
-                wraw[(n, h)] = t
 
-        brow = const.tile([P, GRP], BF16, name="brow")
-        nc.vector.memset(brow[:], 0.0)
-        nc.scalar.dma_start(out=brow[0:4, :], in_=bq.rearrange("(j n) -> j n", n=GRP))
-        nc.scalar.dma_start(out=brow[4:8, :], in_=bk.rearrange("(j n) -> j n", n=GRP))
-
-        load_x(0)
-        load_x(1)
-        load_w(0)
-        load_x(2)
-        load_x(3)
-        load_w(1)
-        load_w(2)
+        for s in range(4 + RAW_BUFS):
+            load(s)
 
         zero_col = const.tile([P, 1], F32, name="zero_col")
         nc.vector.memset(zero_col[:], 0.0)
@@ -115,213 +130,168 @@ def tile_densemha_pa_kernel(tc, hidden_states, Wq, bq, Wk, bk, out_0, out_1):
         neg_c = const.tile([P, NT], F32, name="neg_c")
         nc.vector.scalar_tensor_tensor(out=neg_c[:], in0=quart[:], scalar=0.5, in1=quart[:], op0=ALU.is_gt, op1=ALU.subtract)
 
-        cos_t = const.tile([P, N_TOK, 1, DH], F32, name="cos_t")
-        sin_t = const.tile([P, N_TOK, 1, DH], F32, name="sin_t")
+        cos_tm = const.tile([P, N_TOK, DH], F32, name="cos_tm")
+        sin_tm = const.tile([P, N_TOK, DH], F32, name="sin_tm")
         ns3 = neg_s[:].rearrange("p (a i) -> p a i", a=N_TOK)
         nc3 = neg_c[:].rearrange("p (a i) -> p a i", a=N_TOK)
         two_pi = 2.0 * math.pi
-        nc.scalar.activation(out=sin_t[:, :, 0, 0:HALF], in_=ns3, func=ACT.Sin, scale=two_pi)
-        nc.scalar.activation(out=sin_t[:, :, 0, HALF:DH], in_=ns3, func=ACT.Sin, scale=-two_pi)
-        nc.scalar.activation(out=cos_t[:, :, 0, 0:HALF], in_=nc3, func=ACT.Sin, scale=-two_pi)
-        nc.scalar.activation(out=cos_t[:, :, 0, HALF:DH], in_=nc3, func=ACT.Sin, scale=-two_pi)
+        for lo in (0, HALF):
+            nc.scalar.activation(out=sin_tm[:, :, lo:lo + HALF], in_=ns3, func=ACT.Sin, scale=-two_pi)
+            nc.scalar.activation(out=cos_tm[:, :, lo:lo + HALF], in_=nc3, func=ACT.Sin, scale=-two_pi)
 
-        bias_sb = const.tile([P, N_GRP, GRP], F32, name="bias_sb")
+        bcol = const.tile([P, 32], F32, name="bcol")
 
-        def bias_bcast(n):
-            bank = tp_pool.tile([P, GRP], F32, name="bank")
-            nc.tensor.matmul(out=bank[:], lhsT=ident_bf[:, n:n + 1].to_broadcast([P, P]), rhs=brow[:], start=True, stop=True)
-            nc.scalar.copy(out=bias_sb[:, n, :], in_=bank[:])
+        def bias_columns():
+            bank = tp_pool.tile([P, P], BF16, name="bank")
+            nc.tensor.transpose(bank[:], zrows[:], ident_bf[:])
+            nc.vector.tensor_copy(out=bcol[:], in_=bank[:, 0:32])
 
-        def transpose_unit(blocks):
-            grouped = grp_pool.tile([P, 4, P, 4], BF16, name="grouped", align_bytes=64)
+        cos_fm = const.tile([P, S], F32, name="cos_fm")
+        sin_fm = const.tile([P, S], F32, name="sin_fm")
+        nsin_fm = const.tile([P, S], F32, name="nsin_fm")
+
+        def turn_tables():
+            for src, dst in ((cos_tm, cos_fm), (sin_tm, sin_fm)):
+                bank = tp_pool.tile([P, N_TOK, P], F32, name="bank")
+                for a in range(N_TOK):
+                    nc.tensor.transpose(bank[:, a, :], src[:, a, :], ident[:])
+                nc.scalar.copy(out=dst[:], in_=bank[:].rearrange("p a t -> p (a t)"))
+            nc.vector.tensor_scalar(out=nsin_fm[:], in0=sin_fm[:], scalar1=-1.0, scalar2=None, op0=ALU.mult)
+
+        def it_unit(words, c0, permute):
+            if permute:
+                grouped = grp_pool.tile([P, 2, 2, 2, HALF, 4], BF16, name="grouped", align_bytes=64)
+            else:
+                grouped = grp_pool.tile([P, 2, 2, P, 4], BF16, name="grouped", align_bytes=64)
             gw = grouped[:].bitcast(F32)
-            for half in range(2):
+            for j in range(2):
                 bank = tp_pool.tile([P, 2, 2, P], F32, name="bank")
                 for s in range(2):
                     for u in range(2):
-                        nc.tensor.transpose(bank[:, s, u, :], blocks[2 * half + s][:, u::2], ident[:])
-                nc.scalar.copy(out=gw[:, 2 * half:2 * half + 2, :, :], in_=bank[:].rearrange("p s u r -> p s r u"))
-            return grouped
-
-        def quantize(grouped, codes, scales):
-            nc.vector.quantize_mx(out=codes.bitcast(FP8X4), scales=scales, in_=grouped[:].rearrange("p b r j -> p (b r j)"))
+                        nc.tensor.transpose(bank[:, s, u, :], words[:, 2 * j + s, c0 + u:c0 + 256:2], ident[:])
+                if permute:
+                    nc.scalar.copy(
+                        out=gw[:, j].rearrange("p y x r u -> p x y r u"),
+                        in_=bank[:].rearrange("p x u (y r) -> p x y r u", y=2),
+                    )
+                else:
+                    nc.scalar.copy(out=gw[:, j], in_=bank[:].rearrange("p s u r -> p s r u"))
+            if permute:
+                return grouped[:].rearrange("p a b c r j -> p (a b c r j)")
+            return grouped[:].rearrange("p a b r j -> p (a b r j)")
 
         xq = {}
         xs = {}
-        xg = {}
-
-        def tr_x(a):
-            words = xraw[a][:].bitcast(F32)
-            xg[a] = transpose_unit([words[:, 256 * g:256 * (g + 1)] for g in range(N_PASS)])
-
-        def qz_x(a):
-            xq[a] = const.tile([P, N_PASS * P], U32, name="xq%d" % a, align_bytes=64)
-            xs[a] = const.tile([P, N_PASS * P], U8, name="xs%d" % a, align_bytes=64)
-            quantize(xg[a], xq[a][:], xs[a][:])
-
         wq = {}
         ws = {}
-        wg = {}
+        flat = {}
 
-        def tr_w(n, g):
-            if n >= N_GRP:
+        def it(s):
+            if s < 0 or s >= N_SEQ:
                 return
-            if g == 0:
-                bias_bcast(n)
-            words = wraw[(n, g // 2)][:].bitcast(F32)
-            c0 = 256 * (g % 2)
-            wg[(n, g)] = transpose_unit([words[:, t, c0:c0 + 256] for t in range(4)])
+            n, h = seq_src(s)
+            for e in range(2):
+                t, c0 = raw[(s, e)]
+                flat[(s, e)] = it_unit(t[:].bitcast(F32), c0, n >= 0)
+            if s >= 4:
+                load(s + RAW_BUFS)
 
-        def qz_w(n, g):
-            if n >= N_GRP:
+        def qz(s, e):
+            if s < 0 or s >= N_SEQ:
                 return
-            if g == 0:
-                wq[n] = wcode_pool.tile([P, N_PASS, GRP], U32, name="wq", align_bytes=64)
-                ws[n] = wcode_pool.tile([P, N_PASS, GRP], U8, name="ws", align_bytes=64)
-            quantize(wg[(n, g)], wq[n][:, g, :], ws[n][:, g, :])
+            n, h = seq_src(s)
+            g = 2 * h + e
+            if n < 0:
+                xq[g] = const.tile([P, S], U32, name="xq%d" % g, align_bytes=64)
+                xs[g] = const.tile([P, S], U8, name="xs%d" % g, align_bytes=64)
+                codes, scales = xq[g][:], xs[g][:]
+            else:
+                if g == 0:
+                    wq[n] = wcode_pool.tile([P, N_PASS, GRP], U32, name="wq", align_bytes=64)
+                    ws[n] = wcode_pool.tile([P, N_PASS, GRP], U8, name="ws", align_bytes=64)
+                codes, scales = wq[n][:, g, :], ws[n][:, g, :]
+            nc.vector.quantize_mx(out=codes.bitcast(FP8X4), scales=scales, in_=flat[(s, e)])
 
         acc = {}
 
-        def mm(n, a):
-            if n >= N_GRP:
+        def mx(q):
+            if q < 0 or q >= N_PAIR:
                 return
-            t = acc_pool.tile([P, GRP], F32, name="acc")
-            acc[(n, a)] = t
-            for g in range(N_PASS):
-                cols = slice(g * P, (g + 1) * P)
-                nc.tensor.matmul_mx(
-                    out=t[:],
-                    lhsT=xq[a][:, cols].bitcast(FP8X4),
-                    lhsT_scale=xs[a][:, cols],
-                    rhs=wq[n][:, g, :].bitcast(FP8X4),
-                    rhs_scale=ws[n][:, g, :],
-                    start=(g == 0),
-                    stop=(g == N_PASS - 1),
+            n, pi = q // 2, q % 2
+            for y in range(2):
+                t = acc_pool.tile([P, S], F32, name="acc")
+                acc[(q, y)] = t
+                cols = slice((2 * pi + y) * P, (2 * pi + y + 1) * P)
+                for g in range(N_PASS):
+                    nc.tensor.matmul_mx(
+                        out=t[:],
+                        lhsT=wq[n][:, g, cols].bitcast(FP8X4),
+                        lhsT_scale=ws[n][:, g, cols],
+                        rhs=xq[g][:].bitcast(FP8X4),
+                        rhs_scale=xs[g][:],
+                        start=(g == 0),
+                        stop=(g == N_PASS - 1),
+                    )
+
+        ucs = {}
+        uss = {}
+
+        def stt(q):
+            if q < 0 or q >= N_PAIR:
+                return
+            n, pi = q // 2, q % 2
+            m = (n % 4) * 2 + pi
+            c_a = (n // 4) * 16 + m
+            c_b = c_a + 8
+            uc = ep_pool.tile([P, 2, S], F32, name="uc")
+            us = ep_pool.tile([P, 2, S], F32, name="us")
+            ucs[q], uss[q] = uc, us
+            for out, y, col, table in (
+                (uc[:, 0, :], 0, c_a, cos_fm), (us[:, 1, :], 0, c_a, sin_fm),
+                (uc[:, 1, :], 1, c_b, cos_fm), (us[:, 0, :], 1, c_b, nsin_fm),
+            ):
+                nc.vector.scalar_tensor_tensor(
+                    out=out, in0=acc[(q, y)][:], scalar=bcol[:, col:col + 1], in1=table[:], op0=ALU.add, op1=ALU.mult
                 )
 
-        ys = {}
-        rots = {}
-        ress = {}
+        def add(q):
+            if q < 0 or q >= N_PAIR:
+                return
+            nc.vector.tensor_tensor(out=ucs[q][:], in0=ucs[q][:], in1=uss[q][:], op=ALU.add)
 
-        def ep_tiles(n):
-            ys[n] = ep_pool.tile([P, N_TOK, 4, DH], F32, name="y")
-            rots[n] = ep_pool.tile([P, N_TOK, 4, DH], F32, name="rot")
-            ress[n] = ep_pool.tile([P, N_TOK, 4, DH], F32, name="res")
-
-        def add_bias(n, a):
-            nc.vector.tensor_tensor(
-                out=ys[n][:, a, :, :].rearrange("p h f -> p (h f)"), in0=acc[(n, a)][:], in1=bias_sb[:, n, :], op=ALU.add
-            )
-
-        def rope_mul(n, a0, a1):
-            y, rot, res = ys[n], rots[n], ress[n]
-            k = a1 - a0
-            nc.vector.tensor_tensor(
-                out=rot[:, a0:a1, :, 0:HALF], in0=y[:, a0:a1, :, HALF:DH],
-                in1=sin_t[:, a0:a1, :, 0:HALF].to_broadcast([P, k, 4, HALF]), op=ALU.mult,
-            )
-            nc.vector.tensor_tensor(
-                out=rot[:, a0:a1, :, HALF:DH], in0=y[:, a0:a1, :, 0:HALF],
-                in1=sin_t[:, a0:a1, :, HALF:DH].to_broadcast([P, k, 4, HALF]), op=ALU.mult,
-            )
-            nc.vector.tensor_tensor(
-                out=res[:, a0:a1, :, :], in0=y[:, a0:a1, :, :],
-                in1=cos_t[:, a0:a1, :, :].to_broadcast([P, k, 4, DH]), op=ALU.mult,
-            )
-
-        def rope_add(n, a0, a1):
-            rot, res = rots[n], ress[n]
-            nc.vector.tensor_tensor(out=res[:, a0:a1, :, :], in0=res[:, a0:a1, :, :], in1=rot[:, a0:a1, :, :], op=ALU.add)
+        def ot(q):
+            if q < 0 or q >= N_PAIR:
+                return
+            n, pi = q // 2, q % 2
+            uc = ucs[q]
+            res = ep_pool.tile([P, N_TOK, 2, 2, HALF], F32, name="res")
+            for j in range(2):
+                bank = tp_pool.tile([P, 2, 2, P], F32, name="bank")
+                for a2 in range(2):
+                    a = 2 * j + a2
+                    for y in range(2):
+                        nc.tensor.transpose(bank[:, a2, y, :], uc[:, y, a * P:(a + 1) * P], ident[:])
+                for a2 in range(2):
+                    nc.scalar.copy(
+                        out=res[:, 2 * j + a2].rearrange("p x y r -> p y x r"),
+                        in_=bank[:, a2].rearrange("p y (x r) -> p y x r", x=2),
+                    )
             dst = out_0 if n < 4 else out_1
-            h0 = 4 * (n % 4)
-            for a in range(a0, a1):
+            for x in range(2):
+                head = 4 * (n % 4) + 2 * pi + x
                 nc.sync.dma_start(
-                    out=dst[0, h0:h0 + 4, a * P:(a + 1) * P, :].rearrange("h p f -> p h f"), in_=res[:, a, :, :]
+                    out=dst[0, head].rearrange("(a p) f -> p a f", p=P),
+                    in_=res[:, :, x].rearrange("p a y r -> p a (y r)"),
                 )
 
-        tr_x(0)
-        tr_x(1)
-        tr_w(0, 0)
-        qz_x(0)
-        tr_w(0, 1)
-        qz_x(1)
-        tr_w(0, 2)
-        qz_w(0, 0)
-        tr_w(0, 3)
-        qz_w(0, 1)
-        tr_x(2)
-        qz_w(0, 2)
-        tr_x(3)
-        qz_w(0, 3)
-        qz_x(2)
-        qz_x(3)
-
-        ep_tiles(0)
-        mm(0, 0)
-        mm(0, 1)
-        add_bias(0, 0)
-        mm(0, 2)
-        rope_mul(0, 0, 1)
-        add_bias(0, 1)
-        mm(0, 3)
-        rope_add(0, 0, 1)
-        rope_mul(0, 1, 2)
-        tr_w(1, 0)
-        tr_w(1, 1)
-        add_bias(0, 2)
-        rope_add(0, 1, 2)
-        qz_w(1, 0)
-        rope_mul(0, 2, 3)
-        add_bias(0, 3)
-        tr_w(1, 2)
-        tr_w(1, 3)
-        rope_add(0, 2, 3)
-        qz_w(1, 1)
-        rope_mul(0, 3, 4)
-        qz_w(1, 2)
-        rope_add(0, 3, 4)
-        qz_w(1, 3)
-        load_w(3)
-        tr_w(2, 0)
-        tr_w(2, 1)
-        mm(1, 0)
-        mm(1, 1)
-        qz_w(2, 0)
-        tr_w(2, 2)
-        tr_w(2, 3)
-        qz_w(2, 1)
-        mm(1, 2)
-        mm(1, 3)
-        qz_w(2, 2)
-        qz_w(2, 3)
-
-        for c in range(1, N_GRP):
-            if c + 3 < N_GRP:
-                load_w(c + 3)
-            ep_tiles(c)
-            tr_w(c + 2, 0)
-            tr_w(c + 2, 1)
-            for a in range(N_TOK):
-                add_bias(c, a)
-            qz_w(c + 2, 0)
-            mm(c + 1, 0)
-            mm(c + 1, 1)
-            if c < N_GRP - 1:
-                rope_mul(c, 0, 4)
-                tr_w(c + 2, 2)
-                tr_w(c + 2, 3)
-                qz_w(c + 2, 1)
-                rope_add(c, 0, 4)
-                mm(c + 1, 2)
-                mm(c + 1, 3)
-                qz_w(c + 2, 2)
-                qz_w(c + 2, 3)
-            else:
-                rope_mul(c, 0, 1)
-                rope_mul(c, 1, 2)
-                rope_add(c, 0, 1)
-                rope_mul(c, 2, 3)
-                rope_add(c, 1, 2)
-                rope_mul(c, 3, 4)
-                rope_add(c, 2, 3)
-                rope_add(c, 3, 4)
+        for q in range(-5, N_PAIR + 2):
+            ot(q - 2)
+            stt(q - 1)
+            mx(q)
+            qz(q + 4, 0)
+            it(q + 5)
+            if q == -2:
+                bias_columns()
+                turn_tables()
+            add(q - 1)
+            qz(q + 4, 1)

@@ -23,7 +23,8 @@ N_PASS = 4
 N_GRP = 8
 GRP = 512
 N_PAIR = 16
-RAW_BUFS = 6
+T_ADD = (14, 15)
+RAW_BUFS = 5
 ROPE_BASE = 10000.0
 FLOPS = 2 * S * HID * 2 * HID
 
@@ -34,6 +35,7 @@ def tile_densemha_pa_kernel(tc, hidden_states, Wq, bq, Wk, bk, out_0, out_1):
         const = ctx.enter_context(tc.tile_pool(name="const", bufs=1))
         head_pool = ctx.enter_context(tc.tile_pool(name="head", bufs=8))
         raw_pool = ctx.enter_context(tc.tile_pool(name="raw", bufs=RAW_BUFS))
+        dw_pool = ctx.enter_context(tc.tile_pool(name="dw", bufs=4))
         grp_pool = ctx.enter_context(tc.tile_pool(name="grp", bufs=6))
         wcode_pool = ctx.enter_context(tc.tile_pool(name="wcode", bufs=3))
         ep_pool = ctx.enter_context(tc.tile_pool(name="ep", bufs=3))
@@ -65,12 +67,11 @@ def tile_densemha_pa_kernel(tc, hidden_states, Wq, bq, Wk, bk, out_0, out_1):
                 for e in range(2):
                     t = head_pool.tile([P, 4, GRP], BF16, name="wh")
                     nc.sync.dma_start(out=t[:], in_=view[:, :, e * GRP:(e + 1) * GRP])
-                    raw[(s, e)] = (t, 0)
+                    raw[(s, e)] = t
             else:
                 t = raw_pool.tile([P, 4, HID // 2], BF16, name="wr")
                 nc.sync.dma_start(out=t[:], in_=view)
-                raw[(s, 0)] = (t, 0)
-                raw[(s, 1)] = (t, 256)
+                raw[(s, 0)] = t
 
         zrows = const.tile([P, P], BF16, name="zrows")
         nc.vector.memset(zrows[:], 0.0)
@@ -158,7 +159,23 @@ def tile_densemha_pa_kernel(tc, hidden_states, Wq, bq, Wk, bk, out_0, out_1):
                 nc.scalar.copy(out=dst[:], in_=bank[:].rearrange("p a t -> p (a t)"))
             nc.vector.tensor_scalar(out=nsin_fm[:], in0=sin_fm[:], scalar1=-1.0, scalar2=None, op0=ALU.mult)
 
-        def it_unit(words, c0, permute):
+        def split_words(src, dst, t0, t1, copy):
+            copy(
+                out=dst[:, t0:t1, :].rearrange("p t (e u w) -> p t e u w", u=2, w=P),
+                in_=src[:, t0:t1, :].rearrange("p t (e w u) -> p t e u w", u=2, w=P),
+            )
+
+        dwords = {}
+
+        def deint(s):
+            if s < 0 or s >= N_SEQ:
+                return
+            if s >= 4:
+                d = dw_pool.tile([P, 2, 512], F32, name="dw")
+                split_words(raw[(s, 0)][:].bitcast(F32), d, 0, 2, nc.scalar.copy)
+                dwords[s] = d
+
+        def it_unit(words, split, c0, permute):
             if permute:
                 grouped = grp_pool.tile([P, 2, 2, 2, HALF, 4], BF16, name="grouped", align_bytes=64)
             else:
@@ -168,7 +185,11 @@ def tile_densemha_pa_kernel(tc, hidden_states, Wq, bq, Wk, bk, out_0, out_1):
                 bank = tp_pool.tile([P, 2, 2, P], F32, name="bank")
                 for s in range(2):
                     for u in range(2):
-                        nc.tensor.transpose(bank[:, s, u, :], words[:, 2 * j + s, c0 + u:c0 + 256:2], ident[:])
+                        if j == 0 and split is not None:
+                            src = split[:, s, c0 + u * P:c0 + (u + 1) * P]
+                        else:
+                            src = words[:, 2 * j + s, c0 + u:c0 + 256:2]
+                        nc.tensor.transpose(bank[:, s, u, :], src, ident[:])
                 if permute:
                     nc.scalar.copy(
                         out=gw[:, j].rearrange("p y x r u -> p x y r u"),
@@ -191,8 +212,10 @@ def tile_densemha_pa_kernel(tc, hidden_states, Wq, bq, Wk, bk, out_0, out_1):
                 return
             n, h = seq_src(s)
             for e in range(2):
-                t, c0 = raw[(s, e)]
-                flat[(s, e)] = it_unit(t[:].bitcast(F32), c0, n >= 0)
+                if s < 4:
+                    flat[(s, e)] = it_unit(raw[(s, e)][:].bitcast(F32), None, 0, n >= 0)
+                else:
+                    flat[(s, e)] = it_unit(raw[(s, 0)][:].bitcast(F32), dwords[s], 256 * e, n >= 0)
             if s >= 4:
                 load(s + RAW_BUFS)
 
@@ -255,7 +278,7 @@ def tile_densemha_pa_kernel(tc, hidden_states, Wq, bq, Wk, bk, out_0, out_1):
                 )
 
         def add(q):
-            if q < 0 or q >= N_PAIR:
+            if q < 0 or q >= N_PAIR or q in T_ADD:
                 return
             nc.vector.tensor_tensor(out=ucs[q][:], in0=ucs[q][:], in1=uss[q][:], op=ALU.add)
 
@@ -270,7 +293,12 @@ def tile_densemha_pa_kernel(tc, hidden_states, Wq, bq, Wk, bk, out_0, out_1):
                 for a2 in range(2):
                     a = 2 * j + a2
                     for y in range(2):
-                        nc.tensor.transpose(bank[:, a2, y, :], uc[:, y, a * P:(a + 1) * P], ident[:])
+                        cols = slice(a * P, (a + 1) * P)
+                        if q in T_ADD:
+                            nc.tensor.matmul(out=bank[:, a2, y, :], lhsT=uc[:, y, cols], rhs=ident[:], is_transpose=True, start=True, stop=False)
+                            nc.tensor.matmul(out=bank[:, a2, y, :], lhsT=uss[q][:, y, cols], rhs=ident[:], is_transpose=True, start=False, stop=True)
+                        else:
+                            nc.tensor.transpose(bank[:, a2, y, :], uc[:, y, cols], ident[:])
                 for a2 in range(2):
                     nc.scalar.copy(
                         out=res[:, 2 * j + a2].rearrange("p x y r -> p y x r"),
@@ -284,14 +312,16 @@ def tile_densemha_pa_kernel(tc, hidden_states, Wq, bq, Wk, bk, out_0, out_1):
                     in_=res[:, :, x].rearrange("p a y r -> p a (y r)"),
                 )
 
-        for q in range(-5, N_PAIR + 2):
-            ot(q - 2)
-            stt(q - 1)
-            mx(q)
-            qz(q + 4, 0)
-            it(q + 5)
-            if q == -2:
-                bias_columns()
-                turn_tables()
-            add(q - 1)
-            qz(q + 4, 1)
+        with tc.manual_schedule(engines={mybir.EngineType.PE}):
+            for q in range(-6, N_PAIR + 2):
+                ot(q - 2)
+                stt(q - 1)
+                mx(q)
+                qz(q + 4, 0)
+                it(q + 5)
+                deint(q + 6)
+                if q == -2:
+                    bias_columns()
+                    turn_tables()
+                add(q - 1)
+                qz(q + 4, 1)

@@ -24,7 +24,8 @@ N_GRP = 8
 GRP = 512
 N_PAIR = 16
 T_ADD = (14, 15)
-RAW_BUFS = 5
+RAW_BUFS = 4
+OT_LAG = 3
 ROPE_BASE = 10000.0
 FLOPS = 2 * S * HID * 2 * HID
 
@@ -35,10 +36,10 @@ def tile_densemha_pa_kernel(tc, hidden_states, Wq, bq, Wk, bk, out_0, out_1):
         const = ctx.enter_context(tc.tile_pool(name="const", bufs=1))
         head_pool = ctx.enter_context(tc.tile_pool(name="head", bufs=8))
         raw_pool = ctx.enter_context(tc.tile_pool(name="raw", bufs=RAW_BUFS))
-        dw_pool = ctx.enter_context(tc.tile_pool(name="dw", bufs=4))
+        dw_pool = ctx.enter_context(tc.tile_pool(name="dw", bufs=3))
         grp_pool = ctx.enter_context(tc.tile_pool(name="grp", bufs=6))
         wcode_pool = ctx.enter_context(tc.tile_pool(name="wcode", bufs=3))
-        ep_pool = ctx.enter_context(tc.tile_pool(name="ep", bufs=3))
+        ep_pool = ctx.enter_context(tc.tile_pool(name="ep", bufs=5))
         tp_pool = ctx.enter_context(tc.psum_pool(name="tp", bufs=4))
         acc_pool = ctx.enter_context(tc.psum_pool(name="acc", bufs=4))
 
@@ -167,13 +168,18 @@ def tile_densemha_pa_kernel(tc, hidden_states, Wq, bq, Wk, bk, out_0, out_1):
 
         dwords = {}
 
-        def deint(s):
-            if s < 0 or s >= N_SEQ:
+        def deint_s(s):
+            if s < 4 or s >= N_SEQ:
                 return
-            if s >= 4:
-                d = dw_pool.tile([P, 2, 512], F32, name="dw")
-                split_words(raw[(s, 0)][:].bitcast(F32), d, 0, 2, nc.scalar.copy)
-                dwords[s] = d
+            d = dw_pool.tile([P, 4, 512], F32, name="dw")
+            split_words(raw[(s, 0)][:].bitcast(F32), d, 0, 2, nc.scalar.copy)
+            dwords[s] = d
+
+        def deint_v(s):
+            if s < 4 or s >= N_SEQ:
+                return
+            split_words(raw[(s, 0)][:].bitcast(F32), dwords[s], 2, 4, nc.vector.tensor_copy)
+            load(s + RAW_BUFS)
 
         def it_unit(words, split, c0, permute):
             if permute:
@@ -185,8 +191,8 @@ def tile_densemha_pa_kernel(tc, hidden_states, Wq, bq, Wk, bk, out_0, out_1):
                 bank = tp_pool.tile([P, 2, 2, P], F32, name="bank")
                 for s in range(2):
                     for u in range(2):
-                        if j == 0 and split is not None:
-                            src = split[:, s, c0 + u * P:c0 + (u + 1) * P]
+                        if split is not None:
+                            src = split[:, 2 * j + s, c0 + u * P:c0 + (u + 1) * P]
                         else:
                             src = words[:, 2 * j + s, c0 + u:c0 + 256:2]
                         nc.tensor.transpose(bank[:, s, u, :], src, ident[:])
@@ -215,9 +221,7 @@ def tile_densemha_pa_kernel(tc, hidden_states, Wq, bq, Wk, bk, out_0, out_1):
                 if s < 4:
                     flat[(s, e)] = it_unit(raw[(s, e)][:].bitcast(F32), None, 0, n >= 0)
                 else:
-                    flat[(s, e)] = it_unit(raw[(s, 0)][:].bitcast(F32), dwords[s], 256 * e, n >= 0)
-            if s >= 4:
-                load(s + RAW_BUFS)
+                    flat[(s, e)] = it_unit(None, dwords[s], 256 * e, n >= 0)
 
         def qz(s, e):
             if s < 0 or s >= N_SEQ:
@@ -259,20 +263,21 @@ def tile_densemha_pa_kernel(tc, hidden_states, Wq, bq, Wk, bk, out_0, out_1):
         ucs = {}
         uss = {}
 
-        def stt(q):
+        def stt(q, first, last):
             if q < 0 or q >= N_PAIR:
                 return
             n, pi = q // 2, q % 2
             m = (n % 4) * 2 + pi
             c_a = (n // 4) * 16 + m
             c_b = c_a + 8
-            uc = ep_pool.tile([P, 2, S], F32, name="uc")
-            us = ep_pool.tile([P, 2, S], F32, name="us")
-            ucs[q], uss[q] = uc, us
+            if first == 0:
+                ucs[q] = ep_pool.tile([P, 2, S], F32, name="uc")
+                uss[q] = ep_pool.tile([P, 2, S], F32, name="us")
+            uc, us = ucs[q], uss[q]
             for out, y, col, table in (
                 (uc[:, 0, :], 0, c_a, cos_fm), (us[:, 1, :], 0, c_a, sin_fm),
                 (uc[:, 1, :], 1, c_b, cos_fm), (us[:, 0, :], 1, c_b, nsin_fm),
-            ):
+            )[first:last]:
                 nc.vector.scalar_tensor_tensor(
                     out=out, in0=acc[(q, y)][:], scalar=bcol[:, col:col + 1], in1=table[:], op0=ALU.add, op1=ALU.mult
                 )
@@ -280,16 +285,18 @@ def tile_densemha_pa_kernel(tc, hidden_states, Wq, bq, Wk, bk, out_0, out_1):
         def add(q):
             if q < 0 or q >= N_PAIR or q in T_ADD:
                 return
-            nc.vector.tensor_tensor(out=ucs[q][:], in0=ucs[q][:], in1=uss[q][:], op=ALU.add)
+            nc.gpsimd.tensor_tensor(out=ucs[q][:], in0=ucs[q][:], in1=uss[q][:], op=ALU.add)
 
-        def ot(q):
+        banks = {}
+        ress = {}
+
+        def ot_t(q):
             if q < 0 or q >= N_PAIR:
                 return
-            n, pi = q // 2, q % 2
             uc = ucs[q]
-            res = ep_pool.tile([P, N_TOK, 2, 2, HALF], F32, name="res")
             for j in range(2):
                 bank = tp_pool.tile([P, 2, 2, P], F32, name="bank")
+                banks[(q, j)] = bank
                 for a2 in range(2):
                     a = 2 * j + a2
                     for y in range(2):
@@ -299,10 +306,17 @@ def tile_densemha_pa_kernel(tc, hidden_states, Wq, bq, Wk, bk, out_0, out_1):
                             nc.tensor.matmul(out=bank[:, a2, y, :], lhsT=uss[q][:, y, cols], rhs=ident[:], is_transpose=True, start=False, stop=True)
                         else:
                             nc.tensor.transpose(bank[:, a2, y, :], uc[:, y, cols], ident[:])
+
+        def ot_e(q):
+            if q < 0 or q >= N_PAIR:
+                return
+            n, pi = q // 2, q % 2
+            res = ep_pool.tile([P, N_TOK, 2, 2, HALF], F32, name="res")
+            for j in range(2):
                 for a2 in range(2):
                     nc.scalar.copy(
                         out=res[:, 2 * j + a2].rearrange("p x y r -> p y x r"),
-                        in_=bank[:, a2].rearrange("p y (x r) -> p y x r", x=2),
+                        in_=banks[(q, j)][:, a2].rearrange("p y (x r) -> p y x r", x=2),
                     )
             dst = out_0 if n < 4 else out_1
             for x in range(2):
@@ -312,16 +326,20 @@ def tile_densemha_pa_kernel(tc, hidden_states, Wq, bq, Wk, bk, out_0, out_1):
                     in_=res[:, :, x].rearrange("p a y r -> p a (y r)"),
                 )
 
-        with tc.manual_schedule(engines={mybir.EngineType.PE}):
-            for q in range(-6, N_PAIR + 2):
-                ot(q - 2)
-                stt(q - 1)
+        ET = mybir.EngineType
+        with tc.manual_schedule(engines={ET.PE, ET.DVE, ET.Pool, ET.Activation}):
+            for q in range(-6, N_PAIR + OT_LAG):
+                ot_t(q - OT_LAG)
+                ot_e(q - OT_LAG)
+                stt(q - 1, 0, 3)
                 mx(q)
                 qz(q + 4, 0)
+                deint_s(q + 6)
+                deint_v(q + 6)
+                qz(q + 4, 1)
+                stt(q - 1, 3, 4)
+                add(q - 1)
                 it(q + 5)
-                deint(q + 6)
                 if q == -2:
                     bias_columns()
                     turn_tables()
-                add(q - 1)
-                qz(q + 4, 1)

@@ -213,15 +213,14 @@ def tile_densemha_pa_kernel(tc, hidden_states, Wq, bq, Wk, bk, out_0, out_1):
         ws = {}
         flat = {}
 
-        def it(s):
+        def it(s, e):
             if s < 0 or s >= N_SEQ:
                 return
             n, h = seq_src(s)
-            for e in range(2):
-                if s < 4:
-                    flat[(s, e)] = it_unit(raw[(s, e)][:].bitcast(F32), None, 0, n >= 0)
-                else:
-                    flat[(s, e)] = it_unit(None, dwords[s], 256 * e, n >= 0)
+            if s < 4:
+                flat[(s, e)] = it_unit(raw[(s, e)][:].bitcast(F32), None, 0, n >= 0)
+            else:
+                flat[(s, e)] = it_unit(None, dwords[s], 256 * e, n >= 0)
 
         def qz(s, e):
             if s < 0 or s >= N_SEQ:
@@ -241,24 +240,23 @@ def tile_densemha_pa_kernel(tc, hidden_states, Wq, bq, Wk, bk, out_0, out_1):
 
         acc = {}
 
-        def mx(q):
+        def mx(q, y):
             if q < 0 or q >= N_PAIR:
                 return
             n, pi = q // 2, q % 2
-            for y in range(2):
-                t = acc_pool.tile([P, S], F32, name="acc")
-                acc[(q, y)] = t
-                cols = slice((2 * pi + y) * P, (2 * pi + y + 1) * P)
-                for g in range(N_PASS):
-                    nc.tensor.matmul_mx(
-                        out=t[:],
-                        lhsT=wq[n][:, g, cols].bitcast(FP8X4),
-                        lhsT_scale=ws[n][:, g, cols],
-                        rhs=xq[g][:].bitcast(FP8X4),
-                        rhs_scale=xs[g][:],
-                        start=(g == 0),
-                        stop=(g == N_PASS - 1),
-                    )
+            t = acc_pool.tile([P, S], F32, name="acc")
+            acc[(q, y)] = t
+            cols = slice((2 * pi + y) * P, (2 * pi + y + 1) * P)
+            for g in range(N_PASS):
+                nc.tensor.matmul_mx(
+                    out=t[:],
+                    lhsT=wq[n][:, g, cols].bitcast(FP8X4),
+                    lhsT_scale=ws[n][:, g, cols],
+                    rhs=xq[g][:].bitcast(FP8X4),
+                    rhs_scale=xs[g][:],
+                    start=(g == 0),
+                    stop=(g == N_PASS - 1),
+                )
 
         ucs = {}
         uss = {}
@@ -290,34 +288,36 @@ def tile_densemha_pa_kernel(tc, hidden_states, Wq, bq, Wk, bk, out_0, out_1):
         banks = {}
         ress = {}
 
-        def ot_t(q):
+        def ot_t(q, j):
             if q < 0 or q >= N_PAIR:
                 return
             uc = ucs[q]
-            for j in range(2):
-                bank = tp_pool.tile([P, 2, 2, P], F32, name="bank")
-                banks[(q, j)] = bank
-                for a2 in range(2):
-                    a = 2 * j + a2
-                    for y in range(2):
-                        cols = slice(a * P, (a + 1) * P)
-                        if q in T_ADD:
-                            nc.tensor.matmul(out=bank[:, a2, y, :], lhsT=uc[:, y, cols], rhs=ident[:], is_transpose=True, start=True, stop=False)
-                            nc.tensor.matmul(out=bank[:, a2, y, :], lhsT=uss[q][:, y, cols], rhs=ident[:], is_transpose=True, start=False, stop=True)
-                        else:
-                            nc.tensor.transpose(bank[:, a2, y, :], uc[:, y, cols], ident[:])
+            bank = tp_pool.tile([P, 2, 2, P], F32, name="bank")
+            banks[(q, j)] = bank
+            for a2 in range(2):
+                a = 2 * j + a2
+                for y in range(2):
+                    cols = slice(a * P, (a + 1) * P)
+                    if q in T_ADD:
+                        nc.tensor.matmul(out=bank[:, a2, y, :], lhsT=uc[:, y, cols], rhs=ident[:], is_transpose=True, start=True, stop=False)
+                        nc.tensor.matmul(out=bank[:, a2, y, :], lhsT=uss[q][:, y, cols], rhs=ident[:], is_transpose=True, start=False, stop=True)
+                    else:
+                        nc.tensor.transpose(bank[:, a2, y, :], uc[:, y, cols], ident[:])
 
-        def ot_e(q):
+        def ot_e(q, j):
             if q < 0 or q >= N_PAIR:
                 return
             n, pi = q // 2, q % 2
-            res = ep_pool.tile([P, N_TOK, 2, 2, HALF], F32, name="res")
-            for j in range(2):
-                for a2 in range(2):
-                    nc.scalar.copy(
-                        out=res[:, 2 * j + a2].rearrange("p x y r -> p y x r"),
-                        in_=banks[(q, j)][:, a2].rearrange("p y (x r) -> p y x r", x=2),
-                    )
+            if j == 0:
+                ress[q] = ep_pool.tile([P, N_TOK, 2, 2, HALF], F32, name="res")
+            res = ress[q]
+            for a2 in range(2):
+                nc.scalar.copy(
+                    out=res[:, 2 * j + a2].rearrange("p x y r -> p y x r"),
+                    in_=banks[(q, j)][:, a2].rearrange("p y (x r) -> p y x r", x=2),
+                )
+            if j == 0:
+                return
             dst = out_0 if n < 4 else out_1
             for x in range(2):
                 head = 4 * (n % 4) + 2 * pi + x
@@ -329,17 +329,21 @@ def tile_densemha_pa_kernel(tc, hidden_states, Wq, bq, Wk, bk, out_0, out_1):
         ET = mybir.EngineType
         with tc.manual_schedule(engines={ET.PE, ET.DVE, ET.Pool, ET.Activation}):
             for q in range(-6, N_PAIR + OT_LAG):
-                ot_t(q - OT_LAG)
-                ot_e(q - OT_LAG)
+                ot_t(q - OT_LAG, 0)
+                ot_e(q - OT_LAG, 0)
+                it(q + 4, 1)
                 stt(q - 1, 0, 3)
-                mx(q)
+                mx(q, 0)
                 qz(q + 4, 0)
                 deint_s(q + 6)
                 deint_v(q + 6)
+                ot_t(q - OT_LAG, 1)
+                ot_e(q - OT_LAG, 1)
+                it(q + 5, 0)
+                mx(q, 1)
                 qz(q + 4, 1)
                 stt(q - 1, 3, 4)
                 add(q - 1)
-                it(q + 5)
                 if q == -2:
                     bias_columns()
                     turn_tables()

@@ -20,12 +20,11 @@ DH = 128
 HALF = 64
 N_TOK = 4
 N_PASS = 4
-N_GRP = 8
-GRP = 512
 N_PAIR = 16
+PAIR = 256
 T_ADD = (14, 15)
-RAW_BUFS = 4
-OT_LAG = 3
+N_DIRECT = 4
+RAW_BUFS = 5
 ROPE_BASE = 10000.0
 FLOPS = 2 * S * HID * 2 * HID
 
@@ -38,41 +37,41 @@ def tile_densemha_pa_kernel(tc, hidden_states, Wq, bq, Wk, bk, out_0, out_1):
         raw_pool = ctx.enter_context(tc.tile_pool(name="raw", bufs=RAW_BUFS))
         dw_pool = ctx.enter_context(tc.tile_pool(name="dw", bufs=3))
         grp_pool = ctx.enter_context(tc.tile_pool(name="grp", bufs=6))
-        wcode_pool = ctx.enter_context(tc.tile_pool(name="wcode", bufs=3))
-        ep_pool = ctx.enter_context(tc.tile_pool(name="ep", bufs=5))
+        wcode_pool = ctx.enter_context(tc.tile_pool(name="wcode", bufs=4))
+        uc_pool = ctx.enter_context(tc.tile_pool(name="ucp", bufs=5))
+        us_pool = ctx.enter_context(tc.tile_pool(name="usp", bufs=5))
+        res_pool = ctx.enter_context(tc.tile_pool(name="resp", bufs=3))
         tp_pool = ctx.enter_context(tc.psum_pool(name="tp", bufs=4))
         acc_pool = ctx.enter_context(tc.psum_pool(name="acc", bufs=4))
 
-        def seq_src(s):
-            if s == 0 or s == 2:
-                return (-1, s // 2)
-            if s == 1 or s == 3:
-                return (0, s // 2)
-            return ((s - 2) // 2, s % 2)
+        xraw = {}
+        wraw = {}
 
-        N_SEQ = 2 * N_GRP + 2
-        raw = {}
+        def load_x(g):
+            t = head_pool.tile([P, N_TOK, 512], BF16, name="hd")
+            nc.sync.dma_start(
+                out=t[:], in_=hidden_states[0, :, g * 512:(g + 1) * 512].rearrange("(p t) k -> p t k", t=N_TOK)
+            )
+            xraw[g] = t
 
-        def load(s):
-            if s >= N_SEQ:
+        def w_rows(s):
+            w = Wq if s < 8 else Wk
+            r0 = (s % 8) * PAIR
+            return w[r0:r0 + PAIR, :].rearrange("(x p) k -> p x k", p=P)
+
+        def load_w(s):
+            if s >= N_PAIR:
                 return
-            n, h = seq_src(s)
-            if n < 0:
-                rows = hidden_states[0, :, h * 1024:(h + 1) * 1024]
+            view = w_rows(s)
+            if s < N_DIRECT:
+                for h in range(2):
+                    t = head_pool.tile([P, 2, 1024], BF16, name="hd")
+                    nc.sync.dma_start(out=t[:], in_=view[:, :, h * 1024:(h + 1) * 1024])
+                    wraw[(s, h)] = t
             else:
-                w = Wq if n < 4 else Wk
-                r0 = (n % 4) * GRP
-                rows = w[r0:r0 + GRP, h * 1024:(h + 1) * 1024]
-            view = rows.rearrange("(t p) k -> p t k", p=P)
-            if s < 4:
-                for e in range(2):
-                    t = head_pool.tile([P, 4, GRP], BF16, name="wh")
-                    nc.sync.dma_start(out=t[:], in_=view[:, :, e * GRP:(e + 1) * GRP])
-                    raw[(s, e)] = t
-            else:
-                t = raw_pool.tile([P, 4, HID // 2], BF16, name="wr")
+                t = raw_pool.tile([P, 2, HID], BF16, name="wr")
                 nc.sync.dma_start(out=t[:], in_=view)
-                raw[(s, 0)] = t
+                wraw[s] = t
 
         zrows = const.tile([P, P], BF16, name="zrows")
         nc.vector.memset(zrows[:], 0.0)
@@ -84,8 +83,10 @@ def tile_densemha_pa_kernel(tc, hidden_states, Wq, bq, Wk, bk, out_0, out_1):
                     out=zrows[r0:r0 + 8, :].rearrange("m (x r) -> m x r", x=2), in_=bv[:, y].rearrange("x m r -> m x r")
                 )
 
-        for s in range(4 + RAW_BUFS):
-            load(s)
+        for g in range(N_PASS):
+            load_x(g)
+        for s in range(2):
+            load_w(s)
 
         zero_col = const.tile([P, 1], F32, name="zero_col")
         nc.vector.memset(zero_col[:], 0.0)
@@ -96,9 +97,11 @@ def tile_densemha_pa_kernel(tc, hidden_states, Wq, bq, Wk, bk, out_0, out_1):
         make_identity(nc, ident[:])
         ident_bf = const.tile([P, P], BF16, name="ident_bf")
         make_identity(nc, ident_bf[:])
+        junk_u = const.tile([P, 1], U32, name="junk_u")
+        junk_f = const.tile([P, 1], F32, name="junk_f")
 
         tpos_i = const.tile([P, N_TOK], I32, name="tpos_i")
-        nc.gpsimd.iota(tpos_i[:], pattern=[[P, N_TOK]], base=0, channel_multiplier=1)
+        nc.gpsimd.iota(tpos_i[:], pattern=[[1, N_TOK]], base=0, channel_multiplier=N_TOK)
         tpos = const.tile([P, N_TOK], F32, name="tpos")
         nc.vector.tensor_copy(out=tpos[:], in_=tpos_i[:])
         one_col = const.tile([P, 1], F32, name="one_col")
@@ -157,55 +160,31 @@ def tile_densemha_pa_kernel(tc, hidden_states, Wq, bq, Wk, bk, out_0, out_1):
                 bank = tp_pool.tile([P, N_TOK, P], F32, name="bank")
                 for a in range(N_TOK):
                     nc.tensor.transpose(bank[:, a, :], src[:, a, :], ident[:])
-                nc.scalar.copy(out=dst[:], in_=bank[:].rearrange("p a t -> p (a t)"))
+                nc.vector.tensor_copy(out=dst[:], in_=bank[:].rearrange("p a t -> p (a t)"))
             nc.vector.tensor_scalar(out=nsin_fm[:], in0=sin_fm[:], scalar1=-1.0, scalar2=None, op0=ALU.mult)
 
-        def split_words(src, dst, t0, t1, copy):
-            copy(
-                out=dst[:, t0:t1, :].rearrange("p t (e u w) -> p t e u w", u=2, w=P),
-                in_=src[:, t0:t1, :].rearrange("p t (e w u) -> p t e u w", u=2, w=P),
-            )
-
+        port = {"last": None}
         dwords = {}
 
-        def deint_s(s):
-            if s < 4 or s >= N_SEQ:
-                return
-            d = dw_pool.tile([P, 4, 512], F32, name="dw")
-            split_words(raw[(s, 0)][:].bitcast(F32), d, 0, 2, nc.scalar.copy)
-            dwords[s] = d
-
         def deint_v(s):
-            if s < 4 or s >= N_SEQ:
+            if s < N_DIRECT or s >= N_PAIR:
                 return
-            split_words(raw[(s, 0)][:].bitcast(F32), dwords[s], 2, 4, nc.vector.tensor_copy)
-            load(s + RAW_BUFS)
+            d = dw_pool.tile([P, 2, N_PASS, 2, P], F32, name="dw")
+            dwords[s] = d
+            words = wraw[s][:].bitcast(F32)
+            nc.vector.tensor_copy(
+                out=d[:, :, 1:N_PASS], in_=words[:, :, 256:1024].rearrange("p x (g w u) -> p x g u w", u=2, w=P)
+            )
+            port["last"] = (junk_f, d[:, 1, N_PASS - 1, 1, P - 1:P])
 
-        def it_unit(words, split, c0, permute):
-            if permute:
-                grouped = grp_pool.tile([P, 2, 2, 2, HALF, 4], BF16, name="grouped", align_bytes=64)
-            else:
-                grouped = grp_pool.tile([P, 2, 2, P, 4], BF16, name="grouped", align_bytes=64)
-            gw = grouped[:].bitcast(F32)
-            for j in range(2):
-                bank = tp_pool.tile([P, 2, 2, P], F32, name="bank")
-                for s in range(2):
-                    for u in range(2):
-                        if split is not None:
-                            src = split[:, 2 * j + s, c0 + u * P:c0 + (u + 1) * P]
-                        else:
-                            src = words[:, 2 * j + s, c0 + u:c0 + 256:2]
-                        nc.tensor.transpose(bank[:, s, u, :], src, ident[:])
-                if permute:
-                    nc.scalar.copy(
-                        out=gw[:, j].rearrange("p y x r u -> p x y r u"),
-                        in_=bank[:].rearrange("p x u (y r) -> p x y r u", y=2),
-                    )
-                else:
-                    nc.scalar.copy(out=gw[:, j], in_=bank[:].rearrange("p s u r -> p s r u"))
-            if permute:
-                return grouped[:].rearrange("p a b c r j -> p (a b c r j)")
-            return grouped[:].rearrange("p a b r j -> p (a b r j)")
+        def deint_s(s):
+            if s < N_DIRECT or s >= N_PAIR:
+                return
+            words = wraw[s][:].bitcast(F32)
+            nc.scalar.copy(
+                out=dwords[s][:, :, 0], in_=words[:, :, 0:256].rearrange("p x (w u) -> p x u w", u=2)
+            )
+            load_w(s + RAW_BUFS)
 
         xq = {}
         xs = {}
@@ -213,45 +192,66 @@ def tile_densemha_pa_kernel(tc, hidden_states, Wq, bq, Wk, bk, out_0, out_1):
         ws = {}
         flat = {}
 
-        def it(s, e):
-            if s < 0 or s >= N_SEQ:
-                return
-            n, h = seq_src(s)
-            if s < 4:
-                flat[(s, e)] = it_unit(raw[(s, e)][:].bitcast(F32), None, 0, n >= 0)
-            else:
-                flat[(s, e)] = it_unit(None, dwords[s], 256 * e, n >= 0)
+        def xt(g):
+            grouped = grp_pool.tile([P, 2, 2, P, 4], BF16, name="grouped", align_bytes=64)
+            gw = grouped[:].bitcast(F32)
+            words = xraw[g][:].bitcast(F32)
+            for j in range(2):
+                bank = tp_pool.tile([P, 2, 2, P], F32, name="bank")
+                for s in range(2):
+                    for u in range(2):
+                        nc.tensor.transpose(bank[:, s, u, :], words[:, 2 * j + s, u:256:2], ident[:])
+                nc.scalar.copy(out=gw[:, j], in_=bank[:].rearrange("p s u r -> p s r u"))
+            flat[("x", g)] = grouped[:].rearrange("p a b r j -> p (a b r j)")
 
-        def qz(s, e):
-            if s < 0 or s >= N_SEQ:
+        def xqz(g):
+            xq[g] = const.tile([P, S], U32, name="xq%d" % g, align_bytes=64)
+            xs[g] = const.tile([P, S], U8, name="xs%d" % g, align_bytes=64)
+            nc.vector.quantize_mx(out=xq[g][:].bitcast(FP8X4), scales=xs[g][:], in_=flat[("x", g)])
+
+        def it(s, h):
+            if s < 0 or s >= N_PAIR:
                 return
-            n, h = seq_src(s)
-            g = 2 * h + e
-            if n < 0:
-                xq[g] = const.tile([P, S], U32, name="xq%d" % g, align_bytes=64)
-                xs[g] = const.tile([P, S], U8, name="xs%d" % g, align_bytes=64)
-                codes, scales = xq[g][:], xs[g][:]
-            else:
-                if g == 0:
-                    wq[n] = wcode_pool.tile([P, N_PASS, GRP], U32, name="wq", align_bytes=64)
-                    ws[n] = wcode_pool.tile([P, N_PASS, GRP], U8, name="ws", align_bytes=64)
-                codes, scales = wq[n][:, g, :], ws[n][:, g, :]
-            nc.vector.quantize_mx(out=codes.bitcast(FP8X4), scales=scales, in_=flat[(s, e)])
+            grouped = grp_pool.tile([P, 2, 2, 2, HALF, 4], BF16, name="grouped", align_bytes=64)
+            gw = grouped[:].bitcast(F32)
+            for g2 in range(2):
+                bank = tp_pool.tile([P, 2, 2, P], F32, name="bank")
+                for x in range(2):
+                    for u in range(2):
+                        if s < N_DIRECT:
+                            src = wraw[(s, h)][:].bitcast(F32)[:, x, g2 * 256 + u:(g2 + 1) * 256:2]
+                        else:
+                            src = dwords[s][:, x, 2 * h + g2, u, :]
+                        nc.tensor.transpose(bank[:, x, u, :], src, ident[:])
+                nc.scalar.copy(
+                    out=gw[:, g2].rearrange("p y x r u -> p x y r u"),
+                    in_=bank[:].rearrange("p x u (y r) -> p x y r u", y=2),
+                )
+            flat[(s, h)] = grouped[:].rearrange("p a b c r j -> p (a b c r j)")
+
+        def qz(s, h):
+            if s < 0 or s >= N_PAIR:
+                return
+            if h == 0:
+                wq[s] = wcode_pool.tile([P, N_PASS * PAIR], U32, name="wq", align_bytes=64)
+                ws[s] = wcode_pool.tile([P, N_PASS * PAIR], U8, name="ws", align_bytes=64)
+            cols = slice(h * 2 * PAIR, (h + 1) * 2 * PAIR)
+            nc.vector.quantize_mx(out=wq[s][:, cols].bitcast(FP8X4), scales=ws[s][:, cols], in_=flat[(s, h)])
+            port["last"] = (junk_u, wq[s][:, (h + 1) * 2 * PAIR - 1:(h + 1) * 2 * PAIR])
 
         acc = {}
 
         def mx(q, y):
             if q < 0 or q >= N_PAIR:
                 return
-            n, pi = q // 2, q % 2
             t = acc_pool.tile([P, S], F32, name="acc")
             acc[(q, y)] = t
-            cols = slice((2 * pi + y) * P, (2 * pi + y + 1) * P)
             for g in range(N_PASS):
+                cols = slice(g * PAIR + y * P, g * PAIR + (y + 1) * P)
                 nc.tensor.matmul_mx(
                     out=t[:],
-                    lhsT=wq[n][:, g, cols].bitcast(FP8X4),
-                    lhsT_scale=ws[n][:, g, cols],
+                    lhsT=wq[q][:, cols].bitcast(FP8X4),
+                    lhsT_scale=ws[q][:, cols],
                     rhs=xq[g][:].bitcast(FP8X4),
                     rhs_scale=xs[g][:],
                     start=(g == 0),
@@ -261,89 +261,86 @@ def tile_densemha_pa_kernel(tc, hidden_states, Wq, bq, Wk, bk, out_0, out_1):
         ucs = {}
         uss = {}
 
-        def stt(q, first, last):
+        def stt(q, y):
             if q < 0 or q >= N_PAIR:
                 return
-            n, pi = q // 2, q % 2
-            m = (n % 4) * 2 + pi
-            c_a = (n // 4) * 16 + m
-            c_b = c_a + 8
-            if first == 0:
-                ucs[q] = ep_pool.tile([P, 2, S], F32, name="uc")
-                uss[q] = ep_pool.tile([P, 2, S], F32, name="us")
-            uc, us = ucs[q], uss[q]
-            for out, y, col, table in (
-                (uc[:, 0, :], 0, c_a, cos_fm), (us[:, 1, :], 0, c_a, sin_fm),
-                (uc[:, 1, :], 1, c_b, cos_fm), (us[:, 0, :], 1, c_b, nsin_fm),
-            )[first:last]:
-                nc.vector.scalar_tensor_tensor(
-                    out=out, in0=acc[(q, y)][:], scalar=bcol[:, col:col + 1], in1=table[:], op0=ALU.add, op1=ALU.mult
-                )
+            col = (q // 8) * 16 + y * 8 + q % 8
+            if y == 0:
+                ucs[q] = uc_pool.tile([P, 2, S], F32, name="uc")
+                uss[q] = us_pool.tile([P, 2, S], F32, name="us")
+            n_cut = 2 if (q == N_PAIR - 1 and y == 1) else 1
+            width = S // n_cut
+            for c in range(n_cut):
+                cols = slice(c * width, (c + 1) * width)
+                for out, table in ((ucs[q][:, y, cols], cos_fm), (uss[q][:, 1 - y, cols], sin_fm if y == 0 else nsin_fm)):
+                    nc.vector.scalar_tensor_tensor(
+                        out=out, in0=acc[(q, y)][:, cols], scalar=bcol[:, col:col + 1], in1=table[:, cols],
+                        op0=ALU.add, op1=ALU.mult,
+                    )
 
-        def add(q):
+        def add(q, j):
             if q < 0 or q >= N_PAIR or q in T_ADD:
                 return
-            nc.gpsimd.tensor_tensor(out=ucs[q][:], in0=ucs[q][:], in1=uss[q][:], op=ALU.add)
+            if port["last"] is not None:
+                nc.gpsimd.tensor_copy(out=port["last"][0][:], in_=port["last"][1])
+            cols = slice(j * 2 * P, (j + 1) * 2 * P)
+            nc.gpsimd.tensor_tensor(out=ucs[q][:, :, cols], in0=ucs[q][:, :, cols], in1=uss[q][:, :, cols], op=ALU.add)
 
         banks = {}
         ress = {}
 
-        def ot_t(q, j):
+        def ot(q, j):
             if q < 0 or q >= N_PAIR:
                 return
             uc = ucs[q]
             bank = tp_pool.tile([P, 2, 2, P], F32, name="bank")
-            banks[(q, j)] = bank
             for a2 in range(2):
-                a = 2 * j + a2
+                cols = slice((2 * j + a2) * P, (2 * j + a2 + 1) * P)
                 for y in range(2):
-                    cols = slice(a * P, (a + 1) * P)
                     if q in T_ADD:
                         nc.tensor.matmul(out=bank[:, a2, y, :], lhsT=uc[:, y, cols], rhs=ident[:], is_transpose=True, start=True, stop=False)
                         nc.tensor.matmul(out=bank[:, a2, y, :], lhsT=uss[q][:, y, cols], rhs=ident[:], is_transpose=True, start=False, stop=True)
                     else:
                         nc.tensor.transpose(bank[:, a2, y, :], uc[:, y, cols], ident[:])
-
-        def ot_e(q, j):
-            if q < 0 or q >= N_PAIR:
-                return
-            n, pi = q // 2, q % 2
             if j == 0:
-                ress[q] = ep_pool.tile([P, N_TOK, 2, 2, HALF], F32, name="res")
+                ress[q] = res_pool.tile([P, 2, N_TOK, 2, HALF], F32, name="res")
             res = ress[q]
-            for a2 in range(2):
-                nc.scalar.copy(
-                    out=res[:, 2 * j + a2].rearrange("p x y r -> p y x r"),
-                    in_=banks[(q, j)][:, a2].rearrange("p y (x r) -> p y x r", x=2),
-                )
-            if j == 0:
-                return
-            dst = out_0 if n < 4 else out_1
-            for x in range(2):
-                head = 4 * (n % 4) + 2 * pi + x
-                nc.sync.dma_start(
-                    out=dst[0, head].rearrange("(a p) f -> p a f", p=P),
-                    in_=res[:, :, x].rearrange("p a y r -> p a (y r)"),
-                )
+            nc.scalar.copy(
+                out=res[:, :, 2 * j:2 * j + 2].rearrange("p x a y r -> p a y x r"),
+                in_=bank[:].rearrange("p a y (x r) -> p a y x r", x=2),
+            )
+            dst = out_0 if q < 8 else out_1
+            h0 = 2 * (q % 8)
+            rows = dst[0, h0:h0 + 2].rearrange("x (p a) f -> p x a f", a=N_TOK)
+            vals = res[:].rearrange("p x a y r -> p x a (y r)")
+            if q == N_PAIR - 1:
+                nc.sync.dma_start(out=rows[:, :, 2 * j:2 * j + 2, :], in_=vals[:, :, 2 * j:2 * j + 2, :])
+            elif j == 1:
+                nc.sync.dma_start(out=rows, in_=vals)
 
         ET = mybir.EngineType
         with tc.manual_schedule(engines={ET.PE, ET.DVE, ET.Pool, ET.Activation}):
-            for q in range(-6, N_PAIR + OT_LAG):
-                ot_t(q - OT_LAG, 0)
-                ot_e(q - OT_LAG, 0)
-                it(q + 4, 1)
-                stt(q - 1, 0, 3)
+            for g in range(N_PASS):
+                xt(g)
+                if g > 0:
+                    xqz(g - 1)
+            for s in range(2, N_DIRECT + RAW_BUFS):
+                load_w(s)
+            xqz(N_PASS - 1)
+            bias_columns()
+            turn_tables()
+            for q in range(-2, N_PAIR + 3):
+                ot(q - 3, 1)
+                it(q + 1, 1)
+                add(q - 2, 0)
+                stt(q - 1, 1)
+                qz(q + 1, 0)
+                deint_v(q + 3)
                 mx(q, 0)
-                qz(q + 4, 0)
-                deint_s(q + 6)
-                deint_v(q + 6)
-                ot_t(q - OT_LAG, 1)
-                ot_e(q - OT_LAG, 1)
-                it(q + 5, 0)
+                add(q - 2, 1)
+                stt(q, 0)
+                ot(q - 2, 0)
+                it(q + 2, 0)
+                deint_s(q + 3)
                 mx(q, 1)
-                qz(q + 4, 1)
-                stt(q - 1, 3, 4)
-                add(q - 1)
-                if q == -2:
-                    bias_columns()
-                    turn_tables()
+                qz(q + 1, 1)

@@ -22,7 +22,7 @@ N_TOK = 4
 N_PASS = 4
 N_PAIR = 16
 PAIR = 256
-T_ADD = (14, 15)
+T_ADD = (13, 14, 15)
 N_DIRECT = 4
 RAW_BUFS = 5
 ROPE_BASE = 10000.0
@@ -278,13 +278,12 @@ def tile_densemha_pa_kernel(tc, hidden_states, Wq, bq, Wk, bk, out_0, out_1):
                         op0=ALU.add, op1=ALU.mult,
                     )
 
-        def add(q, j):
+        def add(q):
             if q < 0 or q >= N_PAIR or q in T_ADD:
                 return
             if port["last"] is not None:
                 nc.gpsimd.tensor_copy(out=port["last"][0][:], in_=port["last"][1])
-            cols = slice(j * 2 * P, (j + 1) * 2 * P)
-            nc.gpsimd.tensor_tensor(out=ucs[q][:, :, cols], in0=ucs[q][:, :, cols], in1=uss[q][:, :, cols], op=ALU.add)
+            nc.gpsimd.tensor_tensor(out=ucs[q][:], in0=ucs[q][:], in1=uss[q][:], op=ALU.add)
 
         banks = {}
         ress = {}
@@ -329,18 +328,24 @@ def tile_densemha_pa_kernel(tc, hidden_states, Wq, bq, Wk, bk, out_0, out_1):
             xqz(N_PASS - 1)
             bias_columns()
             turn_tables()
-            for q in range(-2, N_PAIR + 3):
-                ot(q - 3, 1)
+            back = {}
+            for p in range(N_PAIR):
+                first = 2 * p + (4 if p in T_ADD else 6)
+                for j in range(2):
+                    back.setdefault(first + j, []).append((p, j))
+            for q in range(-2, N_PAIR + 2):
                 it(q + 1, 1)
-                add(q - 2, 0)
+                for p, j in back.get(2 * q, []):
+                    ot(p, j)
                 stt(q - 1, 1)
                 qz(q + 1, 0)
                 deint_v(q + 3)
                 mx(q, 0)
-                add(q - 2, 1)
-                stt(q, 0)
-                ot(q - 2, 0)
                 it(q + 2, 0)
+                for p, j in back.get(2 * q + 1, []):
+                    ot(p, j)
                 deint_s(q + 3)
-                mx(q, 1)
                 qz(q + 1, 1)
+                add(q - 1)
+                stt(q, 0)
+                mx(q, 1)

@@ -98,7 +98,6 @@ def tile_densemha_pa_kernel(tc, hidden_states, Wq, bq, Wk, bk, out_0, out_1):
         ident_bf = const.tile([P, P], BF16, name="ident_bf")
         make_identity(nc, ident_bf[:])
         junk_u = const.tile([P, 1], U32, name="junk_u")
-        junk_f = const.tile([P, 1], F32, name="junk_f")
 
         tpos_i = const.tile([P, N_TOK], I32, name="tpos_i")
         nc.gpsimd.iota(tpos_i[:], pattern=[[1, N_TOK]], base=0, channel_multiplier=N_TOK)
@@ -166,23 +165,22 @@ def tile_densemha_pa_kernel(tc, hidden_states, Wq, bq, Wk, bk, out_0, out_1):
         port = {"last": None}
         dwords = {}
 
-        def deint_v(s):
-            if s < N_DIRECT or s >= N_PAIR:
-                return
-            d = dw_pool.tile([P, 2, N_PASS, 2, P], F32, name="dw")
-            dwords[s] = d
-            words = wraw[s][:].bitcast(F32)
-            nc.vector.tensor_copy(
-                out=d[:, :, 1:N_PASS], in_=words[:, :, 256:1024].rearrange("p x (g w u) -> p x g u w", u=2, w=P)
-            )
-            port["last"] = (junk_f, d[:, 1, N_PASS - 1, 1, P - 1:P])
-
         def deint_s(s):
             if s < N_DIRECT or s >= N_PAIR:
                 return
+            dwords[s] = dw_pool.tile([P, 2, N_PASS, 2, P], F32, name="dw")
             words = wraw[s][:].bitcast(F32)
             nc.scalar.copy(
                 out=dwords[s][:, :, 0], in_=words[:, :, 0:256].rearrange("p x (w u) -> p x u w", u=2)
+            )
+
+        def deint_v(s):
+            if s < N_DIRECT or s >= N_PAIR:
+                return
+            words = wraw[s][:].bitcast(F32)
+            nc.vector.tensor_copy(
+                out=dwords[s][:, :, 1:N_PASS],
+                in_=words[:, :, 256:1024].rearrange("p x (g w u) -> p x g u w", u=2, w=P),
             )
             load_w(s + RAW_BUFS)
 
@@ -237,7 +235,8 @@ def tile_densemha_pa_kernel(tc, hidden_states, Wq, bq, Wk, bk, out_0, out_1):
                 ws[s] = wcode_pool.tile([P, N_PASS * PAIR], U8, name="ws", align_bytes=64)
             cols = slice(h * 2 * PAIR, (h + 1) * 2 * PAIR)
             nc.vector.quantize_mx(out=wq[s][:, cols].bitcast(FP8X4), scales=ws[s][:, cols], in_=flat[(s, h)])
-            port["last"] = (junk_u, wq[s][:, (h + 1) * 2 * PAIR - 1:(h + 1) * 2 * PAIR])
+            if h == 0:
+                port["last"] = (junk_u, wq[s][:, 2 * PAIR - 1:2 * PAIR])
 
         acc = {}
 
@@ -333,18 +332,23 @@ def tile_densemha_pa_kernel(tc, hidden_states, Wq, bq, Wk, bk, out_0, out_1):
                 first = 2 * p + (4 if p in T_ADD else 6)
                 for j in range(2):
                     back.setdefault(first + j, []).append((p, j))
+            fwd = {}
+            for n in range(2 * N_PAIR):
+                fwd.setdefault(n - (3 if n < 5 else 4), []).append((n // 2, n % 2))
             for q in range(-2, N_PAIR + 2):
-                it(q + 1, 1)
+                for s, h in fwd.get(2 * q, []):
+                    it(s, h)
                 for p, j in back.get(2 * q, []):
                     ot(p, j)
+                deint_s(q + 3)
                 stt(q - 1, 1)
-                qz(q + 1, 0)
                 deint_v(q + 3)
+                qz(q + 1, 0)
                 mx(q, 0)
-                it(q + 2, 0)
+                for s, h in fwd.get(2 * q + 1, []):
+                    it(s, h)
                 for p, j in back.get(2 * q + 1, []):
                     ot(p, j)
-                deint_s(q + 3)
                 qz(q + 1, 1)
                 add(q - 1)
                 stt(q, 0)

@@ -41,8 +41,8 @@ def tile_densemha_pa_kernel(tc, hidden_states, Wq, bq, Wk, bk, out_0, out_1):
         uc_pool = ctx.enter_context(tc.tile_pool(name="ucp", bufs=5))
         us_pool = ctx.enter_context(tc.tile_pool(name="usp", bufs=5))
         res_pool = ctx.enter_context(tc.tile_pool(name="resp", bufs=3))
-        tp_pool = ctx.enter_context(tc.psum_pool(name="tp", bufs=4))
-        acc_pool = ctx.enter_context(tc.psum_pool(name="acc", bufs=4))
+        tp_pool = ctx.enter_context(tc.psum_pool(name="tp", bufs=5))
+        acc_pool = ctx.enter_context(tc.psum_pool(name="acc", bufs=3))
 
         xraw = {}
         wraw = {}

@@ -22,7 +22,7 @@ N_TOK = 4
 N_PASS = 4
 N_PAIR = 16
 PAIR = 256
-T_ADD = (13, 14, 15)
+T_ADD = (14, 15)
 N_DIRECT = 4
 RAW_BUFS = 5
 ROPE_BASE = 10000.0
@@ -171,7 +171,7 @@ def tile_densemha_pa_kernel(tc, hidden_states, Wq, bq, Wk, bk, out_0, out_1):
             dwords[s] = dw_pool.tile([P, 2, N_PASS, 2, P], F32, name="dw")
             words = wraw[s][:].bitcast(F32)
             nc.scalar.copy(
-                out=dwords[s][:, :, 0], in_=words[:, :, 0:256].rearrange("p x (w u) -> p x u w", u=2)
+                out=dwords[s][:, :, N_PASS - 1], in_=words[:, :, 768:1024].rearrange("p x (w u) -> p x u w", u=2)
             )
 
         def deint_v(s):
@@ -179,8 +179,8 @@ def tile_densemha_pa_kernel(tc, hidden_states, Wq, bq, Wk, bk, out_0, out_1):
                 return
             words = wraw[s][:].bitcast(F32)
             nc.vector.tensor_copy(
-                out=dwords[s][:, :, 1:N_PASS],
-                in_=words[:, :, 256:1024].rearrange("p x (g w u) -> p x g u w", u=2, w=P),
+                out=dwords[s][:, :, 0:N_PASS - 1],
+                in_=words[:, :, 0:768].rearrange("p x (g w u) -> p x g u w", u=2, w=P),
             )
             load_w(s + RAW_BUFS)
 
@@ -235,8 +235,8 @@ def tile_densemha_pa_kernel(tc, hidden_states, Wq, bq, Wk, bk, out_0, out_1):
                 ws[s] = wcode_pool.tile([P, N_PASS * PAIR], U8, name="ws", align_bytes=64)
             cols = slice(h * 2 * PAIR, (h + 1) * 2 * PAIR)
             nc.vector.quantize_mx(out=wq[s][:, cols].bitcast(FP8X4), scales=ws[s][:, cols], in_=flat[(s, h)])
-            if h == 0:
-                port["last"] = (junk_u, wq[s][:, 2 * PAIR - 1:2 * PAIR])
+            if h == 1:
+                port["last"] = (junk_u, wq[s][:, 4 * PAIR - 1:4 * PAIR])
 
         acc = {}
 
@@ -329,27 +329,29 @@ def tile_densemha_pa_kernel(tc, hidden_states, Wq, bq, Wk, bk, out_0, out_1):
             turn_tables()
             back = {}
             for p in range(N_PAIR):
-                first = 2 * p + (4 if p in T_ADD else 6)
-                for j in range(2):
-                    back.setdefault(first + j, []).append((p, j))
-            fwd = {}
-            for n in range(2 * N_PAIR):
-                fwd.setdefault(n - (3 if n < 5 else 4), []).append((n // 2, n % 2))
-            for q in range(-2, N_PAIR + 2):
-                for s, h in fwd.get(2 * q, []):
-                    it(s, h)
-                for p, j in back.get(2 * q, []):
-                    ot(p, j)
+                back[p + (2 if p in T_ADD else 3)] = back.get(p + (2 if p in T_ADD else 3), []) + [p]
+            for n in range(4):
+                it(n // 2, n % 2)
+                if n > 0:
+                    qz((n - 1) // 2, (n - 1) % 2)
+            nxt = 4
+            for q in range(0, N_PAIR + 2):
+                due = back.get(q, [])
+                if q > 0:
+                    room = 3 - len(due)
+                    for n in range(nxt, min(nxt + room, 2 * N_PAIR)):
+                        it(n // 2, n % 2)
+                    nxt = min(nxt + room, 2 * N_PAIR)
                 deint_s(q + 3)
-                stt(q - 1, 1)
-                deint_v(q + 3)
-                qz(q + 1, 0)
-                mx(q, 0)
-                for s, h in fwd.get(2 * q + 1, []):
-                    it(s, h)
-                for p, j in back.get(2 * q + 1, []):
-                    ot(p, j)
+                for p in due:
+                    ot(p, 0)
+                    ot(p, 1)
+                if q > 0:
+                    qz(q + 1, 0)
                 qz(q + 1, 1)
+                deint_v(q + 3)
+                mx(q, 0)
+                mx(q, 1)
                 add(q - 1)
                 stt(q, 0)
-                mx(q, 1)
+                stt(q, 1)

@@ -235,8 +235,8 @@ def tile_densemha_pa_kernel(tc, hidden_states, Wq, bq, Wk, bk, out_0, out_1):
                 ws[s] = wcode_pool.tile([P, N_PASS * PAIR], U8, name="ws", align_bytes=64)
             cols = slice(h * 2 * PAIR, (h + 1) * 2 * PAIR)
             nc.vector.quantize_mx(out=wq[s][:, cols].bitcast(FP8X4), scales=ws[s][:, cols], in_=flat[(s, h)])
-            if h == 1:
-                port["last"] = (junk_u, wq[s][:, 4 * PAIR - 1:4 * PAIR])
+            if h == 0:
+                port["last"] = (junk_u, wq[s][:, 2 * PAIR - 1:2 * PAIR])
 
         acc = {}
 

@@ -36,10 +36,9 @@ def tile_densemha_pa_kernel(tc, hidden_states, Wq, bq, Wk, bk, out_0, out_1):
         head_pool = ctx.enter_context(tc.tile_pool(name="head", bufs=8))
         raw_pool = ctx.enter_context(tc.tile_pool(name="raw", bufs=RAW_BUFS))
         dw_pool = ctx.enter_context(tc.tile_pool(name="dw", bufs=3))
-        grp_pool = ctx.enter_context(tc.tile_pool(name="grp", bufs=6))
+        grp_pool = ctx.enter_context(tc.tile_pool(name="grp", bufs=4))
         wcode_pool = ctx.enter_context(tc.tile_pool(name="wcode", bufs=4))
-        uc_pool = ctx.enter_context(tc.tile_pool(name="ucp", bufs=5))
-        us_pool = ctx.enter_context(tc.tile_pool(name="usp", bufs=5))
+        u_pool = ctx.enter_context(tc.tile_pool(name="up", bufs=5))
         res_pool = ctx.enter_context(tc.tile_pool(name="resp", bufs=3))
         tp_pool = ctx.enter_context(tc.psum_pool(name="tp", bufs=5))
         acc_pool = ctx.enter_context(tc.psum_pool(name="acc", bufs=3))
@@ -150,17 +149,17 @@ def tile_densemha_pa_kernel(tc, hidden_states, Wq, bq, Wk, bk, out_0, out_1):
             nc.tensor.transpose(bank[:], zrows[:], ident_bf[:])
             nc.vector.tensor_copy(out=bcol[:], in_=bank[:, 0:32])
 
-        cos_fm = const.tile([P, S], F32, name="cos_fm")
-        sin_fm = const.tile([P, S], F32, name="sin_fm")
-        nsin_fm = const.tile([P, S], F32, name="nsin_fm")
+        tab0 = const.tile([P, 2, S], F32, name="tab0")
+        tab1 = const.tile([P, 2, S], F32, name="tab1")
 
         def turn_tables():
-            for src, dst in ((cos_tm, cos_fm), (sin_tm, sin_fm)):
+            for src, k in ((cos_tm, 0), (sin_tm, 1)):
                 bank = tp_pool.tile([P, N_TOK, P], F32, name="bank")
                 for a in range(N_TOK):
                     nc.tensor.transpose(bank[:, a, :], src[:, a, :], ident[:])
-                nc.vector.tensor_copy(out=dst[:], in_=bank[:].rearrange("p a t -> p (a t)"))
-            nc.vector.tensor_scalar(out=nsin_fm[:], in0=sin_fm[:], scalar1=-1.0, scalar2=None, op0=ALU.mult)
+                nc.vector.tensor_copy(out=tab0[:, k, :], in_=bank[:].rearrange("p a t -> p (a t)"))
+            nc.vector.tensor_copy(out=tab1[:, 0, :], in_=tab0[:, 0, :])
+            nc.vector.tensor_scalar(out=tab1[:, 1, :], in0=tab0[:, 1, :], scalar1=-1.0, scalar2=None, op0=ALU.mult)
 
         port = {"last": None}
         dwords = {}
@@ -189,6 +188,7 @@ def tile_densemha_pa_kernel(tc, hidden_states, Wq, bq, Wk, bk, out_0, out_1):
         wq = {}
         ws = {}
         flat = {}
+        grps = {}
 
         def xt(g):
             grouped = grp_pool.tile([P, 2, 2, P, 4], BF16, name="grouped", align_bytes=64)
@@ -210,33 +210,36 @@ def tile_densemha_pa_kernel(tc, hidden_states, Wq, bq, Wk, bk, out_0, out_1):
         def it(s, h):
             if s < 0 or s >= N_PAIR:
                 return
-            grouped = grp_pool.tile([P, 2, 2, 2, HALF, 4], BF16, name="grouped", align_bytes=64)
-            gw = grouped[:].bitcast(F32)
+            if h == 0:
+                grps[s] = grp_pool.tile([P, 2, 2, 2, 2, HALF, 4], BF16, name="grouped", align_bytes=64)
+                flat[s] = grps[s][:].rearrange("p h a b c r j -> p (h a b c r j)")
+            gw = grps[s][:].bitcast(F32)
             for g2 in range(2):
+                g = 2 * h + g2
                 bank = tp_pool.tile([P, 2, 2, P], F32, name="bank")
                 for x in range(2):
                     for u in range(2):
                         if s < N_DIRECT:
                             src = wraw[(s, h)][:].bitcast(F32)[:, x, g2 * 256 + u:(g2 + 1) * 256:2]
                         else:
-                            src = dwords[s][:, x, 2 * h + g2, u, :]
+                            src = dwords[s][:, x, g, u, :]
                         nc.tensor.transpose(bank[:, x, u, :], src, ident[:])
                 nc.scalar.copy(
-                    out=gw[:, g2].rearrange("p y x r u -> p x y r u"),
+                    out=gw[:, h, g2].rearrange("p y x r u -> p x y r u"),
                     in_=bank[:].rearrange("p x u (y r) -> p x y r u", y=2),
                 )
-            flat[(s, h)] = grouped[:].rearrange("p a b c r j -> p (a b c r j)")
 
-        def qz(s, h):
+        def qz(s, h0, h1):
             if s < 0 or s >= N_PAIR:
                 return
-            if h == 0:
+            if h0 == 0:
                 wq[s] = wcode_pool.tile([P, N_PASS * PAIR], U32, name="wq", align_bytes=64)
                 ws[s] = wcode_pool.tile([P, N_PASS * PAIR], U8, name="ws", align_bytes=64)
-            cols = slice(h * 2 * PAIR, (h + 1) * 2 * PAIR)
-            nc.vector.quantize_mx(out=wq[s][:, cols].bitcast(FP8X4), scales=ws[s][:, cols], in_=flat[(s, h)])
-            if h == 0:
-                port["last"] = (junk_u, wq[s][:, 2 * PAIR - 1:2 * PAIR])
+            cols = slice(h0 * 2 * PAIR, h1 * 2 * PAIR)
+            nc.vector.quantize_mx(
+                out=wq[s][:, cols].bitcast(FP8X4), scales=ws[s][:, cols], in_=flat[s][:, h0 * 8 * PAIR:h1 * 8 * PAIR]
+            )
+            port["last"] = (junk_u, wq[s][:, h1 * 2 * PAIR - 1:h1 * 2 * PAIR])
 
         acc = {}
 
@@ -257,32 +260,32 @@ def tile_densemha_pa_kernel(tc, hidden_states, Wq, bq, Wk, bk, out_0, out_1):
                     stop=(g == N_PASS - 1),
                 )
 
-        ucs = {}
-        uss = {}
+        us4 = {}
 
         def stt(q, y):
             if q < 0 or q >= N_PAIR:
                 return
             col = (q // 8) * 16 + y * 8 + q % 8
             if y == 0:
-                ucs[q] = uc_pool.tile([P, 2, S], F32, name="uc")
-                uss[q] = us_pool.tile([P, 2, S], F32, name="us")
+                us4[q] = u_pool.tile([P, 4, S], F32, name="u4")
+            outs = us4[q][:, 0:4:3, :] if y == 0 else us4[q][:, 1:3, :]
+            table = tab0 if y == 0 else tab1
             n_cut = 2 if (q == N_PAIR - 1 and y == 1) else 1
             width = S // n_cut
             for c in range(n_cut):
                 cols = slice(c * width, (c + 1) * width)
-                for out, table in ((ucs[q][:, y, cols], cos_fm), (uss[q][:, 1 - y, cols], sin_fm if y == 0 else nsin_fm)):
-                    nc.vector.scalar_tensor_tensor(
-                        out=out, in0=acc[(q, y)][:, cols], scalar=bcol[:, col:col + 1], in1=table[:, cols],
-                        op0=ALU.add, op1=ALU.mult,
-                    )
+                nc.vector.scalar_tensor_tensor(
+                    out=outs[:, :, cols],
+                    in0=acc[(q, y)][:, cols].rearrange("p (o t) -> p o t", o=1).to_broadcast([P, 2, width]),
+                    scalar=bcol[:, col:col + 1], in1=table[:, :, cols], op0=ALU.add, op1=ALU.mult,
+                )
 
         def add(q):
             if q < 0 or q >= N_PAIR or q in T_ADD:
                 return
             if port["last"] is not None:
                 nc.gpsimd.tensor_copy(out=port["last"][0][:], in_=port["last"][1])
-            nc.gpsimd.tensor_tensor(out=ucs[q][:], in0=ucs[q][:], in1=uss[q][:], op=ALU.add)
+            nc.gpsimd.tensor_tensor(out=us4[q][:, 0:2, :], in0=us4[q][:, 0:2, :], in1=us4[q][:, 2:4, :], op=ALU.add)
 
         banks = {}
         ress = {}
@@ -290,14 +293,14 @@ def tile_densemha_pa_kernel(tc, hidden_states, Wq, bq, Wk, bk, out_0, out_1):
         def ot(q, j):
             if q < 0 or q >= N_PAIR:
                 return
-            uc = ucs[q]
+            uc = us4[q]
             bank = tp_pool.tile([P, 2, 2, P], F32, name="bank")
             for a2 in range(2):
                 cols = slice((2 * j + a2) * P, (2 * j + a2 + 1) * P)
                 for y in range(2):
                     if q in T_ADD:
                         nc.tensor.matmul(out=bank[:, a2, y, :], lhsT=uc[:, y, cols], rhs=ident[:], is_transpose=True, start=True, stop=False)
-                        nc.tensor.matmul(out=bank[:, a2, y, :], lhsT=uss[q][:, y, cols], rhs=ident[:], is_transpose=True, start=False, stop=True)
+                        nc.tensor.matmul(out=bank[:, a2, y, :], lhsT=uc[:, 2 + y, cols], rhs=ident[:], is_transpose=True, start=False, stop=True)
                     else:
                         nc.tensor.transpose(bank[:, a2, y, :], uc[:, y, cols], ident[:])
             if j == 0:
@@ -333,7 +336,7 @@ def tile_densemha_pa_kernel(tc, hidden_states, Wq, bq, Wk, bk, out_0, out_1):
             for n in range(4):
                 it(n // 2, n % 2)
                 if n > 0:
-                    qz((n - 1) // 2, (n - 1) % 2)
+                    qz((n - 1) // 2, (n - 1) % 2, (n - 1) % 2 + 1)
             nxt = 4
             for q in range(0, N_PAIR + 2):
                 due = back.get(q, [])
@@ -346,9 +349,12 @@ def tile_densemha_pa_kernel(tc, hidden_states, Wq, bq, Wk, bk, out_0, out_1):
                 for p in due:
                     ot(p, 0)
                     ot(p, 1)
-                if q > 0:
-                    qz(q + 1, 0)
-                qz(q + 1, 1)
+                if q + 1 >= N_DIRECT:
+                    qz(q + 1, 0, 2)
+                else:
+                    if q > 0:
+                        qz(q + 1, 0, 1)
+                    qz(q + 1, 1, 2)
                 deint_v(q + 3)
                 mx(q, 0)
                 mx(q, 1)

@@ -23,7 +23,8 @@ N_PASS = 4
 N_PAIR = 16
 PAIR = 256
 T_ADD = (14, 15)
-N_DIRECT = 4
+N_DIRECT = 2
+EARLY_HALVES = {1: 2, 2: 4}
 RAW_BUFS = 5
 ROPE_BASE = 10000.0
 FLOPS = 2 * S * HID * 2 * HID
@@ -167,7 +168,8 @@ def tile_densemha_pa_kernel(tc, hidden_states, Wq, bq, Wk, bk, out_0, out_1):
         def deint_s(s):
             if s < N_DIRECT or s >= N_PAIR:
                 return
-            dwords[s] = dw_pool.tile([P, 2, N_PASS, 2, P], F32, name="dw")
+            if s not in dwords:
+                dwords[s] = dw_pool.tile([P, 2, N_PASS, 2, P], F32, name="dw")
             words = wraw[s][:].bitcast(F32)
             nc.scalar.copy(
                 out=dwords[s][:, :, N_PASS - 1], in_=words[:, :, 768:1024].rearrange("p x (w u) -> p x u w", u=2)
@@ -176,6 +178,8 @@ def tile_densemha_pa_kernel(tc, hidden_states, Wq, bq, Wk, bk, out_0, out_1):
         def deint_v(s):
             if s < N_DIRECT or s >= N_PAIR:
                 return
+            if s not in dwords:
+                dwords[s] = dw_pool.tile([P, 2, N_PASS, 2, P], F32, name="dw")
             words = wraw[s][:].bitcast(F32)
             nc.vector.tensor_copy(
                 out=dwords[s][:, :, 0:N_PASS - 1],
@@ -341,11 +345,17 @@ def tile_densemha_pa_kernel(tc, hidden_states, Wq, bq, Wk, bk, out_0, out_1):
             for q in range(0, N_PAIR + 2):
                 due = back.get(q, [])
                 if q > 0:
-                    room = 3 - len(due)
+                    room = EARLY_HALVES.get(q, 3 - len(due))
                     for n in range(nxt, min(nxt + room, 2 * N_PAIR)):
                         it(n // 2, n % 2)
                     nxt = min(nxt + room, 2 * N_PAIR)
-                deint_s(q + 3)
+                if q == 0:
+                    deint_s(2)
+                elif q == 1:
+                    deint_s(3)
+                    deint_s(4)
+                else:
+                    deint_s(q + 3)
                 for p in due:
                     ot(p, 0)
                     ot(p, 1)
@@ -355,9 +365,11 @@ def tile_densemha_pa_kernel(tc, hidden_states, Wq, bq, Wk, bk, out_0, out_1):
                     if q > 0:
                         qz(q + 1, 0, 1)
                     qz(q + 1, 1, 2)
-                deint_v(q + 3)
+                deint_v(2 if q == 0 else q + 3)
                 mx(q, 0)
                 mx(q, 1)
                 add(q - 1)
                 stt(q, 0)
                 stt(q, 1)
+                if q == 0:
+                    deint_v(3)

@@ -359,13 +359,12 @@ def tile_densemha_pa_kernel(tc, hidden_states, Wq, bq, Wk, bk, out_0, out_1):
                 for p in due:
                     ot(p, 0)
                     ot(p, 1)
-                if q + 1 >= N_DIRECT:
-                    qz(q + 1, 0, 2)
+                if q == 0:
+                    deint_v(2)
+                    qz(1, 1, 2)
                 else:
-                    if q > 0:
-                        qz(q + 1, 0, 1)
-                    qz(q + 1, 1, 2)
-                deint_v(2 if q == 0 else q + 3)
+                    qz(q + 1, 0, 2)
+                    deint_v(q + 3)
                 mx(q, 0)
                 mx(q, 1)
                 add(q - 1)

@@ -47,12 +47,14 @@ def tile_densemha_pa_kernel(tc, hidden_states, Wq, bq, Wk, bk, out_0, out_1):
         xraw = {}
         wraw = {}
 
-        def load_x(g):
-            t = head_pool.tile([P, N_TOK, 512], BF16, name="hd")
-            nc.sync.dma_start(
-                out=t[:], in_=hidden_states[0, :, g * 512:(g + 1) * 512].rearrange("(p t) k -> p t k", t=N_TOK)
-            )
-            xraw[g] = t
+        def load_x(a):
+            t = head_pool.tile([P, HID], BF16, name="hd")
+            rows = hidden_states[0].rearrange("(p t) k -> p t k", t=N_TOK)[:, a, :]
+            n_cut = 2 if a == 0 else 1
+            width = HID // n_cut
+            for c in range(n_cut):
+                nc.sync.dma_start(out=t[:, c * width:(c + 1) * width], in_=rows[:, c * width:(c + 1) * width])
+            xraw[a] = t
 
         def w_rows(s):
             w = Wq if s < 8 else Wk
@@ -83,8 +85,8 @@ def tile_densemha_pa_kernel(tc, hidden_states, Wq, bq, Wk, bk, out_0, out_1):
                     out=zrows[r0:r0 + 8, :].rearrange("m (x r) -> m x r", x=2), in_=bv[:, y].rearrange("x m r -> m x r")
                 )
 
-        for g in range(N_PASS):
-            load_x(g)
+        for a in range(N_TOK):
+            load_x(a)
         for s in range(2):
             load_w(s)
 
@@ -99,49 +101,38 @@ def tile_densemha_pa_kernel(tc, hidden_states, Wq, bq, Wk, bk, out_0, out_1):
         make_identity(nc, ident_bf[:])
         junk_u = const.tile([P, 1], U32, name="junk_u")
 
-        tpos_i = const.tile([P, N_TOK], I32, name="tpos_i")
-        nc.gpsimd.iota(tpos_i[:], pattern=[[1, N_TOK]], base=0, channel_multiplier=N_TOK)
-        tpos = const.tile([P, N_TOK], F32, name="tpos")
-        nc.vector.tensor_copy(out=tpos[:], in_=tpos_i[:])
         one_col = const.tile([P, 1], F32, name="one_col")
         nc.vector.memset(one_col[:], 1.0)
-        freq = const.tile([P, HALF], F32, name="freq")
+        freq = const.tile([P, 2, HALF], F32, name="freq")
         for i in range(8):
             nc.vector.tensor_scalar(
-                out=freq[:, i:i + 1], in0=one_col[:], scalar1=ROPE_BASE ** (-i / 64.0) / (2.0 * math.pi),
+                out=freq[:, 0, i:i + 1], in0=one_col[:], scalar1=ROPE_BASE ** (-i / 64.0) / (2.0 * math.pi),
                 scalar2=None, op0=ALU.mult,
             )
         for j in range(1, 8):
             nc.vector.tensor_scalar(
-                out=freq[:, 8 * j:8 * j + 8], in0=freq[:, 0:8], scalar1=ROPE_BASE ** (-8 * j / 64.0),
+                out=freq[:, 0, 8 * j:8 * j + 8], in0=freq[:, 0, 0:8], scalar1=ROPE_BASE ** (-8 * j / 64.0),
                 scalar2=None, op0=ALU.mult,
             )
-        NT = N_TOK * HALF
-        turns = const.tile([P, NT], F32, name="turns")
-        for a in range(N_TOK):
-            nc.vector.tensor_scalar(
-                out=turns[:, a * HALF:(a + 1) * HALF], in0=freq[:], scalar1=tpos[:, a:a + 1],
-                scalar2=None, op0=ALU.mult,
-            )
-        whole = const.tile([P, NT], I32, name="whole")
+        nc.vector.tensor_copy(out=freq[:, 1, :], in_=freq[:, 0, :])
+        fbank = tp_pool.tile([P, P], F32, name="bank")
+        nc.tensor.transpose(fbank[:], freq[:].rearrange("p x i -> p (x i)"), ident[:])
+        fcol = const.tile([P, 1], F32, name="fcol")
+        nc.vector.tensor_copy(out=fcol[:], in_=fbank[:, 0:1])
+        whole = const.tile([P, S], I32, name="whole")
+        nc.gpsimd.iota(whole[:], pattern=[[1, N_TOK], [N_TOK, P]], base=0, channel_multiplier=0)
+        turns = const.tile([P, S], F32, name="turns")
+        nc.vector.tensor_copy(out=turns[:], in_=whole[:])
+        nc.vector.tensor_scalar(out=turns[:], in0=turns[:], scalar1=fcol[:, 0:1], scalar2=None, op0=ALU.mult)
         nc.vector.tensor_scalar(out=whole[:], in0=turns[:], scalar1=1.0, scalar2=-1.0e-4, op0=ALU.mult, op1=ALU.add)
-        frac = const.tile([P, NT], F32, name="frac")
+        frac = const.tile([P, S], F32, name="frac")
         nc.vector.scalar_tensor_tensor(out=frac[:], in0=whole[:], scalar=-1.0, in1=turns[:], op0=ALU.mult, op1=ALU.add)
-        neg_s = const.tile([P, NT], F32, name="neg_s")
+        neg_s = const.tile([P, S], F32, name="neg_s")
         nc.vector.scalar_tensor_tensor(out=neg_s[:], in0=frac[:], scalar=0.5, in1=frac[:], op0=ALU.is_gt, op1=ALU.subtract)
-        quart = const.tile([P, NT], F32, name="quart")
-        nc.vector.tensor_scalar(out=quart[:], in0=neg_s[:], scalar1=-1.0, scalar2=0.25, op0=ALU.mult, op1=ALU.add)
-        neg_c = const.tile([P, NT], F32, name="neg_c")
-        nc.vector.scalar_tensor_tensor(out=neg_c[:], in0=quart[:], scalar=0.5, in1=quart[:], op0=ALU.is_gt, op1=ALU.subtract)
-
-        cos_tm = const.tile([P, N_TOK, DH], F32, name="cos_tm")
-        sin_tm = const.tile([P, N_TOK, DH], F32, name="sin_tm")
-        ns3 = neg_s[:].rearrange("p (a i) -> p a i", a=N_TOK)
-        nc3 = neg_c[:].rearrange("p (a i) -> p a i", a=N_TOK)
+        nc.vector.tensor_scalar(out=turns[:], in0=neg_s[:], scalar1=-1.0, scalar2=0.25, op0=ALU.mult, op1=ALU.add)
+        neg_c = const.tile([P, S], F32, name="neg_c")
+        nc.vector.scalar_tensor_tensor(out=neg_c[:], in0=turns[:], scalar=0.5, in1=turns[:], op0=ALU.is_gt, op1=ALU.subtract)
         two_pi = 2.0 * math.pi
-        for lo in (0, HALF):
-            nc.scalar.activation(out=sin_tm[:, :, lo:lo + HALF], in_=ns3, func=ACT.Sin, scale=-two_pi)
-            nc.scalar.activation(out=cos_tm[:, :, lo:lo + HALF], in_=nc3, func=ACT.Sin, scale=-two_pi)
 
         bcol = const.tile([P, 32], F32, name="bcol")
 
@@ -153,12 +144,13 @@ def tile_densemha_pa_kernel(tc, hidden_states, Wq, bq, Wk, bk, out_0, out_1):
         tab0 = const.tile([P, 2, S], F32, name="tab0")
         tab1 = const.tile([P, 2, S], F32, name="tab1")
 
-        def turn_tables():
-            for src, k in ((cos_tm, 0), (sin_tm, 1)):
-                bank = tp_pool.tile([P, N_TOK, P], F32, name="bank")
-                for a in range(N_TOK):
-                    nc.tensor.transpose(bank[:, a, :], src[:, a, :], ident[:])
-                nc.vector.tensor_copy(out=tab0[:, k, :], in_=bank[:].rearrange("p a t -> p (a t)"))
+        def table_sin():
+            nc.scalar.activation(out=tab0[:, 1, :], in_=neg_s[:], func=ACT.Sin, scale=-two_pi)
+
+        def table_cos():
+            nc.scalar.activation(out=tab0[:, 0, :], in_=neg_c[:], func=ACT.Sin, scale=-two_pi)
+
+        def second_table():
             nc.vector.tensor_copy(out=tab1[:, 0, :], in_=tab0[:, 0, :])
             nc.vector.tensor_scalar(out=tab1[:, 1, :], in0=tab0[:, 1, :], scalar1=-1.0, scalar2=None, op0=ALU.mult)
 
@@ -194,22 +186,30 @@ def tile_densemha_pa_kernel(tc, hidden_states, Wq, bq, Wk, bk, out_0, out_1):
         flat = {}
         grps = {}
 
-        def xt(g):
-            grouped = grp_pool.tile([P, 2, 2, P, 4], BF16, name="grouped", align_bytes=64)
-            gw = grouped[:].bitcast(F32)
-            words = xraw[g][:].bitcast(F32)
-            for j in range(2):
-                bank = tp_pool.tile([P, 2, 2, P], F32, name="bank")
-                for s in range(2):
-                    for u in range(2):
-                        nc.tensor.transpose(bank[:, s, u, :], words[:, 2 * j + s, u:256:2], ident[:])
-                nc.scalar.copy(out=gw[:, j], in_=bank[:].rearrange("p s u r -> p s r u"))
-            flat[("x", g)] = grouped[:].rearrange("p a b r j -> p (a b r j)")
-
-        def xqz(g):
+        for g in range(N_PASS):
             xq[g] = const.tile([P, S], U32, name="xq%d" % g, align_bytes=64)
             xs[g] = const.tile([P, S], U8, name="xs%d" % g, align_bytes=64)
-            nc.vector.quantize_mx(out=xq[g][:].bitcast(FP8X4), scales=xs[g][:], in_=flat[("x", g)])
+
+        def xt(a):
+            grouped = grp_pool.tile([P, N_PASS, P, 4], BF16, name="grouped", align_bytes=64)
+            gw = grouped[:].bitcast(F32)
+            words = xraw[a][:].bitcast(F32)
+            for j in range(2):
+                bank = tp_pool.tile([P, 2, 2, P], F32, name="bank")
+                for g2 in range(2):
+                    g = 2 * j + g2
+                    for u in range(2):
+                        nc.tensor.transpose(bank[:, g2, u, :], words[:, g * 256 + u:(g + 1) * 256:2], ident[:])
+                nc.scalar.copy(out=gw[:, 2 * j:2 * j + 2], in_=bank[:].rearrange("p g u r -> p g r u"))
+            flat[("x", a)] = grouped
+
+        def xqz(a):
+            cols = slice(a * P, (a + 1) * P)
+            for g in range(N_PASS):
+                nc.vector.quantize_mx(
+                    out=xq[g][:, cols].bitcast(FP8X4), scales=xs[g][:, cols],
+                    in_=flat[("x", a)][:, g].rearrange("p r j -> p (r j)"),
+                )
 
         def it(s, h):
             if s < 0 or s >= N_PAIR:
@@ -333,14 +333,18 @@ def tile_densemha_pa_kernel(tc, hidden_states, Wq, bq, Wk, bk, out_0, out_1):
                 load_w(s)
             xqz(N_PASS - 1)
             bias_columns()
-            turn_tables()
             back = {}
             for p in range(N_PAIR):
                 back[p + (2 if p in T_ADD else 3)] = back.get(p + (2 if p in T_ADD else 3), []) + [p]
             for n in range(4):
                 it(n // 2, n % 2)
+                if n == 1:
+                    table_sin()
+                    table_cos()
                 if n > 0:
                     qz((n - 1) // 2, (n - 1) % 2, (n - 1) % 2 + 1)
+                if n == 2:
+                    second_table()
             nxt = 4
             for q in range(0, N_PAIR + 2):
                 due = back.get(q, [])

@@ -22,7 +22,10 @@ N_TOK = 4
 N_PASS = 4
 N_PAIR = 16
 PAIR = 256
-T_ADD = (14, 15)
+T_ADD = (15,)
+LAG = {15: 1}
+FINE_STORE = (13, 14, 15)
+V_OUT = ((15, 1), (14, 1))
 N_DIRECT = 2
 EARLY_HALVES = {1: 2, 2: 4}
 RAW_BUFS = 5
@@ -310,7 +313,8 @@ def tile_densemha_pa_kernel(tc, hidden_states, Wq, bq, Wk, bk, out_0, out_1):
             if j == 0:
                 ress[q] = res_pool.tile([P, 2, N_TOK, 2, HALF], F32, name="res")
             res = ress[q]
-            nc.scalar.copy(
+            copy_out = nc.vector.tensor_copy if (q, j) in V_OUT else nc.scalar.copy
+            copy_out(
                 out=res[:, :, 2 * j:2 * j + 2].rearrange("p x a y r -> p a y x r"),
                 in_=bank[:].rearrange("p a y (x r) -> p a y x r", x=2),
             )
@@ -318,7 +322,7 @@ def tile_densemha_pa_kernel(tc, hidden_states, Wq, bq, Wk, bk, out_0, out_1):
             h0 = 2 * (q % 8)
             rows = dst[0, h0:h0 + 2].rearrange("x (p a) f -> p x a f", a=N_TOK)
             vals = res[:].rearrange("p x a y r -> p x a (y r)")
-            if q == N_PAIR - 1:
+            if q in FINE_STORE:
                 nc.sync.dma_start(out=rows[:, :, 2 * j:2 * j + 2, :], in_=vals[:, :, 2 * j:2 * j + 2, :])
             elif j == 1:
                 nc.sync.dma_start(out=rows, in_=vals)
@@ -335,7 +339,7 @@ def tile_densemha_pa_kernel(tc, hidden_states, Wq, bq, Wk, bk, out_0, out_1):
             bias_columns()
             back = {}
             for p in range(N_PAIR):
-                back[p + (2 if p in T_ADD else 3)] = back.get(p + (2 if p in T_ADD else 3), []) + [p]
+                back[p + LAG.get(p, 3)] = back.get(p + LAG.get(p, 3), []) + [p]
             for n in range(4):
                 it(n // 2, n % 2)
                 if n == 1:

@@ -29,6 +29,7 @@ V_OUT = ((15, 1), (14, 1))
 N_DIRECT = 2
 EARLY_HALVES = {1: 2, 2: 4}
 RAW_BUFS = 5
+V_PASSES = 2
 ROPE_BASE = 10000.0
 FLOPS = 2 * S * HID * 2 * HID
 
@@ -167,7 +168,8 @@ def tile_densemha_pa_kernel(tc, hidden_states, Wq, bq, Wk, bk, out_0, out_1):
                 dwords[s] = dw_pool.tile([P, 2, N_PASS, 2, P], F32, name="dw")
             words = wraw[s][:].bitcast(F32)
             nc.scalar.copy(
-                out=dwords[s][:, :, N_PASS - 1], in_=words[:, :, 768:1024].rearrange("p x (w u) -> p x u w", u=2)
+                out=dwords[s][:, :, V_PASSES:N_PASS],
+                in_=words[:, :, V_PASSES * 256:1024].rearrange("p x (g w u) -> p x g u w", u=2, w=P),
             )
 
         def deint_v(s):
@@ -177,8 +179,8 @@ def tile_densemha_pa_kernel(tc, hidden_states, Wq, bq, Wk, bk, out_0, out_1):
                 dwords[s] = dw_pool.tile([P, 2, N_PASS, 2, P], F32, name="dw")
             words = wraw[s][:].bitcast(F32)
             nc.vector.tensor_copy(
-                out=dwords[s][:, :, 0:N_PASS - 1],
-                in_=words[:, :, 0:768].rearrange("p x (g w u) -> p x g u w", u=2, w=P),
+                out=dwords[s][:, :, 0:V_PASSES],
+                in_=words[:, :, 0:V_PASSES * 256].rearrange("p x (g w u) -> p x g u w", u=2, w=P),
             )
             load_w(s + RAW_BUFS)
 

@@ -123,19 +123,43 @@ def tile_densemha_pa_kernel(tc, hidden_states, Wq, bq, Wk, bk, out_0, out_1):
         nc.tensor.transpose(fbank[:], freq[:].rearrange("p x i -> p (x i)"), ident[:])
         fcol = const.tile([P, 1], F32, name="fcol")
         nc.vector.tensor_copy(out=fcol[:], in_=fbank[:, 0:1])
+        token = const.tile([P, S], F32, name="token")
+        nc.gpsimd.iota(
+            token[:], pattern=[[1, N_TOK], [N_TOK, P]], base=0, channel_multiplier=0, allow_small_or_imprecise_dtypes=True
+        )
         whole = const.tile([P, S], I32, name="whole")
-        nc.gpsimd.iota(whole[:], pattern=[[1, N_TOK], [N_TOK, P]], base=0, channel_multiplier=0)
         turns = const.tile([P, S], F32, name="turns")
-        nc.vector.tensor_copy(out=turns[:], in_=whole[:])
-        nc.vector.tensor_scalar(out=turns[:], in0=turns[:], scalar1=fcol[:, 0:1], scalar2=None, op0=ALU.mult)
-        nc.vector.tensor_scalar(out=whole[:], in0=turns[:], scalar1=1.0, scalar2=-1.0e-4, op0=ALU.mult, op1=ALU.add)
         frac = const.tile([P, S], F32, name="frac")
-        nc.vector.scalar_tensor_tensor(out=frac[:], in0=whole[:], scalar=-1.0, in1=turns[:], op0=ALU.mult, op1=ALU.add)
         neg_s = const.tile([P, S], F32, name="neg_s")
-        nc.vector.scalar_tensor_tensor(out=neg_s[:], in0=frac[:], scalar=0.5, in1=frac[:], op0=ALU.is_gt, op1=ALU.subtract)
-        nc.vector.tensor_scalar(out=turns[:], in0=neg_s[:], scalar1=-1.0, scalar2=0.25, op0=ALU.mult, op1=ALU.add)
         neg_c = const.tile([P, S], F32, name="neg_c")
-        nc.vector.scalar_tensor_tensor(out=neg_c[:], in0=turns[:], scalar=0.5, in1=turns[:], op0=ALU.is_gt, op1=ALU.subtract)
+        angle_steps = (
+            lambda: nc.vector.tensor_scalar(out=turns[:], in0=token[:], scalar1=fcol[:, 0:1], scalar2=None, op0=ALU.mult),
+            lambda: nc.vector.tensor_scalar(
+                out=whole[:], in0=turns[:], scalar1=1.0, scalar2=-1.0e-4, op0=ALU.mult, op1=ALU.add
+            ),
+            lambda: nc.vector.scalar_tensor_tensor(
+                out=frac[:], in0=whole[:], scalar=-1.0, in1=turns[:], op0=ALU.mult, op1=ALU.add
+            ),
+            lambda: nc.vector.scalar_tensor_tensor(
+                out=neg_s[:], in0=frac[:], scalar=0.5, in1=frac[:], op0=ALU.is_gt, op1=ALU.subtract
+            ),
+            lambda: nc.vector.tensor_scalar(
+                out=turns[:], in0=neg_s[:], scalar1=-1.0, scalar2=0.25, op0=ALU.mult, op1=ALU.add
+            ),
+            lambda: nc.vector.scalar_tensor_tensor(
+                out=neg_c[:], in0=turns[:], scalar=0.5, in1=turns[:], op0=ALU.is_gt, op1=ALU.subtract
+            ),
+        )
+        angle_done = {"n": 0}
+
+        def angle_step():
+            if angle_done["n"] < len(angle_steps):
+                angle_steps[angle_done["n"]]()
+            angle_done["n"] = angle_done["n"] + 1
+
+        for i in range(2):
+            angle_step()
+
         two_pi = 2.0 * math.pi
 
         bcol = const.tile([P, 32], F32, name="bcol")
@@ -215,6 +239,8 @@ def tile_densemha_pa_kernel(tc, hidden_states, Wq, bq, Wk, bk, out_0, out_1):
                     out=xq[g][:, cols].bitcast(FP8X4), scales=xs[g][:, cols],
                     in_=flat[("x", a)][:, g].rearrange("p r j -> p (r j)"),
                 )
+                if g == 1:
+                    angle_step()
 
         def it(s, h):
             if s < 0 or s >= N_PAIR:

import math
from contextlib import ExitStack

import concourse.mybir as mybir
from concourse.masks import make_identity

F32 = mybir.dt.float32
BF16 = mybir.dt.bfloat16
U32 = mybir.dt.uint32
U8 = mybir.dt.uint8
I32 = mybir.dt.int32
FP8X4 = mybir.dt.float8_e5m2_x4
ALU = mybir.AluOpType
ACT = mybir.ActivationFunctionType

P = 128
S = 512
HID = 2048
DH = 128
HALF = 64
N_TOK = 4
N_PASS = 4
N_PAIR = 16
PAIR = 256
T_ADD = (15,)
LAG = {15: 1}
FINE_STORE = (13, 14, 15)
V_OUT = ((15, 1), (14, 1))
N_DIRECT = 2
EARLY_HALVES = {1: 2, 2: 4}
RAW_BUFS = 5
V_PASSES = 2
ROPE_BASE = 10000.0
FLOPS = 2 * S * HID * 2 * HID


def tile_densemha_pa_kernel(tc, hidden_states, Wq, bq, Wk, bk, out_0, out_1):
    nc = tc.nc
    with ExitStack() as ctx:
        const = ctx.enter_context(tc.tile_pool(name="const", bufs=1))
        head_pool = ctx.enter_context(tc.tile_pool(name="head", bufs=8))
        raw_pool = ctx.enter_context(tc.tile_pool(name="raw", bufs=RAW_BUFS))
        dw_pool = ctx.enter_context(tc.tile_pool(name="dw", bufs=3))
        grp_pool = ctx.enter_context(tc.tile_pool(name="grp", bufs=4))
        wcode_pool = ctx.enter_context(tc.tile_pool(name="wcode", bufs=4))
        u_pool = ctx.enter_context(tc.tile_pool(name="up", bufs=5))
        res_pool = ctx.enter_context(tc.tile_pool(name="resp", bufs=3))
        tp_pool = ctx.enter_context(tc.psum_pool(name="tp", bufs=5))
        acc_pool = ctx.enter_context(tc.psum_pool(name="acc", bufs=3))

        xraw = {}
        wraw = {}

        def load_x(a):
            t = head_pool.tile([P, HID], BF16, name="hd")
            rows = hidden_states[0].rearrange("(p t) k -> p t k", t=N_TOK)[:, a, :]
            n_cut = 2 if a == 0 else 1
            width = HID // n_cut
            for c in range(n_cut):
                nc.sync.dma_start(out=t[:, c * width:(c + 1) * width], in_=rows[:, c * width:(c + 1) * width])
            xraw[a] = t

        def w_rows(s):
            w = Wq if s < 8 else Wk
            r0 = (s % 8) * PAIR
            return w[r0:r0 + PAIR, :].rearrange("(x p) k -> p x k", p=P)

        def load_w(s):
            if s >= N_PAIR:
                return
            view = w_rows(s)
            if s < N_DIRECT:
                for h in range(2):
                    t = head_pool.tile([P, 2, 1024], BF16, name="hd")
                    nc.sync.dma_start(out=t[:], in_=view[:, :, h * 1024:(h + 1) * 1024])
                    wraw[(s, h)] = t
            else:
                t = raw_pool.tile([P, 2, HID], BF16, name="wr")
                nc.sync.dma_start(out=t[:], in_=view)
                wraw[s] = t

        zrows = const.tile([P, P], BF16, name="zrows")
        nc.vector.memset(zrows[:], 0.0)
        for v, b in enumerate((bq, bk)):
            bv = b.rearrange("(m x y r) -> x y m r", x=2, y=2, r=HALF)
            for y in range(2):
                r0 = v * 16 + y * 8
                nc.scalar.dma_start(
                    out=zrows[r0:r0 + 8, :].rearrange("m (x r) -> m x r", x=2), in_=bv[:, y].rearrange("x m r -> m x r")
                )

        for a in range(N_TOK):
            load_x(a)
        for s in range(2):
            load_w(s)

        zero_col = const.tile([P, 1], F32, name="zero_col")
        nc.vector.memset(zero_col[:], 0.0)
        warm = const.tile([P, 1], F32, name="warm")
        nc.scalar.activation(out=warm[:], in_=zero_col[:], func=ACT.Sin)

        ident = const.tile([P, P], F32, name="ident")
        make_identity(nc, ident[:])
        ident_bf = const.tile([P, P], BF16, name="ident_bf")
        make_identity(nc, ident_bf[:])
        junk_u = const.tile([P, 1], U32, name="junk_u")

        one_col = const.tile([P, 1], F32, name="one_col")
        nc.vector.memset(one_col[:], 1.0)
        freq = const.tile([P, 2, HALF], F32, name="freq")
        for i in range(8):
            nc.vector.tensor_scalar(
                out=freq[:, 0, i:i + 1], in0=one_col[:], scalar1=ROPE_BASE ** (-i / 64.0) / (2.0 * math.pi),
                scalar2=None, op0=ALU.mult,
            )
        for j in range(1, 8):
            nc.vector.tensor_scalar(
                out=freq[:, 0, 8 * j:8 * j + 8], in0=freq[:, 0, 0:8], scalar1=ROPE_BASE ** (-8 * j / 64.0),
                scalar2=None, op0=ALU.mult,
            )
        nc.vector.tensor_copy(out=freq[:, 1, :], in_=freq[:, 0, :])
        fbank = tp_pool.tile([P, P], F32, name="bank")
        nc.tensor.transpose(fbank[:], freq[:].rearrange("p x i -> p (x i)"), ident[:])
        fcol = const.tile([P, 1], F32, name="fcol")
        nc.vector.tensor_copy(out=fcol[:], in_=fbank[:, 0:1])
        token = const.tile([P, S], F32, name="token")
        nc.gpsimd.iota(
            token[:], pattern=[[1, N_TOK], [N_TOK, P]], base=0, channel_multiplier=0, allow_small_or_imprecise_dtypes=True
        )
        whole = const.tile([P, S], I32, name="whole")
        turns = const.tile([P, S], F32, name="turns")
        frac = const.tile([P, S], F32, name="frac")
        neg_s = const.tile([P, S], F32, name="neg_s")
        neg_c = const.tile([P, S], F32, name="neg_c")
        angle_steps = (
            lambda: nc.vector.tensor_scalar(out=turns[:], in0=token[:], scalar1=fcol[:, 0:1], scalar2=None, op0=ALU.mult),
            lambda: nc.vector.tensor_scalar(
                out=whole[:], in0=turns[:], scalar1=1.0, scalar2=-1.0e-4, op0=ALU.mult, op1=ALU.add
            ),
            lambda: nc.vector.scalar_tensor_tensor(
                out=frac[:], in0=whole[:], scalar=-1.0, in1=turns[:], op0=ALU.mult, op1=ALU.add
            ),
            lambda: nc.vector.scalar_tensor_tensor(
                out=neg_s[:], in0=frac[:], scalar=0.5, in1=frac[:], op0=ALU.is_gt, op1=ALU.subtract
            ),
            lambda: nc.vector.tensor_scalar(
                out=turns[:], in0=neg_s[:], scalar1=-1.0, scalar2=0.25, op0=ALU.mult, op1=ALU.add
            ),
            lambda: nc.vector.scalar_tensor_tensor(
                out=neg_c[:], in0=turns[:], scalar=0.5, in1=turns[:], op0=ALU.is_gt, op1=ALU.subtract
            ),
        )
        angle_done = {"n": 0}

        def angle_step():
            if angle_done["n"] < len(angle_steps):
                angle_steps[angle_done["n"]]()
            angle_done["n"] = angle_done["n"] + 1

        for i in range(2):
            angle_step()

        two_pi = 2.0 * math.pi

        bcol = const.tile([P, 32], F32, name="bcol")

        def bias_columns():
            bank = tp_pool.tile([P, P], BF16, name="bank")
            nc.tensor.transpose(bank[:], zrows[:], ident_bf[:])
            nc.vector.tensor_copy(out=bcol[:], in_=bank[:, 0:32])

        tab0 = const.tile([P, 2, S], F32, name="tab0")
        tab1 = const.tile([P, 2, S], F32, name="tab1")

        def table_sin():
            nc.scalar.activation(out=tab0[:, 1, :], in_=neg_s[:], func=ACT.Sin, scale=-two_pi)

        def table_cos():
            nc.scalar.activation(out=tab0[:, 0, :], in_=neg_c[:], func=ACT.Sin, scale=-two_pi)

        def second_table():
            nc.vector.tensor_copy(out=tab1[:, 0, :], in_=tab0[:, 0, :])
            nc.vector.tensor_scalar(out=tab1[:, 1, :], in0=tab0[:, 1, :], scalar1=-1.0, scalar2=None, op0=ALU.mult)

        port = {"last": None}
        dwords = {}

        def deint_s(s):
            if s < N_DIRECT or s >= N_PAIR:
                return
            if s not in dwords:
                dwords[s] = dw_pool.tile([P, 2, N_PASS, 2, P], F32, name="dw")
            words = wraw[s][:].bitcast(F32)
            nc.scalar.copy(
                out=dwords[s][:, :, V_PASSES:N_PASS],
                in_=words[:, :, V_PASSES * 256:1024].rearrange("p x (g w u) -> p x g u w", u=2, w=P),
            )

        def deint_v(s):
            if s < N_DIRECT or s >= N_PAIR:
                return
            if s not in dwords:
                dwords[s] = dw_pool.tile([P, 2, N_PASS, 2, P], F32, name="dw")
            words = wraw[s][:].bitcast(F32)
            nc.vector.tensor_copy(
                out=dwords[s][:, :, 0:V_PASSES],
                in_=words[:, :, 0:V_PASSES * 256].rearrange("p x (g w u) -> p x g u w", u=2, w=P),
            )
            load_w(s + RAW_BUFS)

        xq = {}
        xs = {}
        wq = {}
        ws = {}
        flat = {}
        grps = {}

        for g in range(N_PASS):
            xq[g] = const.tile([P, S], U32, name="xq%d" % g, align_bytes=64)
            xs[g] = const.tile([P, S], U8, name="xs%d" % g, align_bytes=64)

        def xt(a):
            grouped = grp_pool.tile([P, N_PASS, P, 4], BF16, name="grouped", align_bytes=64)
            gw = grouped[:].bitcast(F32)
            words = xraw[a][:].bitcast(F32)
            for j in range(2):
                bank = tp_pool.tile([P, 2, 2, P], F32, name="bank")
                for g2 in range(2):
                    g = 2 * j + g2
                    for u in range(2):
                        nc.tensor.transpose(bank[:, g2, u, :], words[:, g * 256 + u:(g + 1) * 256:2], ident[:])
                nc.scalar.copy(out=gw[:, 2 * j:2 * j + 2], in_=bank[:].rearrange("p g u r -> p g r u"))
            flat[("x", a)] = grouped

        def xqz(a):
            cols = slice(a * P, (a + 1) * P)
            for g in range(N_PASS):
                nc.vector.quantize_mx(
                    out=xq[g][:, cols].bitcast(FP8X4), scales=xs[g][:, cols],
                    in_=flat[("x", a)][:, g].rearrange("p r j -> p (r j)"),
                )
                if g == 1:
                    angle_step()

        def it(s, h):
            if s < 0 or s >= N_PAIR:
                return
            if h == 0:
                grps[s] = grp_pool.tile([P, 2, 2, 2, 2, HALF, 4], BF16, name="grouped", align_bytes=64)
                flat[s] = grps[s][:].rearrange("p h a b c r j -> p (h a b c r j)")
            gw = grps[s][:].bitcast(F32)
            for g2 in range(2):
                g = 2 * h + g2
                bank = tp_pool.tile([P, 2, 2, P], F32, name="bank")
                for x in range(2):
                    for u in range(2):
                        if s < N_DIRECT:
                            src = wraw[(s, h)][:].bitcast(F32)[:, x, g2 * 256 + u:(g2 + 1) * 256:2]
                        else:
                            src = dwords[s][:, x, g, u, :]
                        nc.tensor.transpose(bank[:, x, u, :], src, ident[:])
                nc.scalar.copy(
                    out=gw[:, h, g2].rearrange("p y x r u -> p x y r u"),
                    in_=bank[:].rearrange("p x u (y r) -> p x y r u", y=2),
                )

        def qz(s, h0, h1):
            if s < 0 or s >= N_PAIR:
                return
            if h0 == 0:
                wq[s] = wcode_pool.tile([P, N_PASS * PAIR], U32, name="wq", align_bytes=64)
                ws[s] = wcode_pool.tile([P, N_PASS * PAIR], U8, name="ws", align_bytes=64)
            cols = slice(h0 * 2 * PAIR, h1 * 2 * PAIR)
            nc.vector.quantize_mx(
                out=wq[s][:, cols].bitcast(FP8X4), scales=ws[s][:, cols], in_=flat[s][:, h0 * 8 * PAIR:h1 * 8 * PAIR]
            )
            port["last"] = (junk_u, wq[s][:, h1 * 2 * PAIR - 1:h1 * 2 * PAIR])

        acc = {}

        def mx(q, y):
            if q < 0 or q >= N_PAIR:
                return
            t = acc_pool.tile([P, S], F32, name="acc")
            acc[(q, y)] = t
            for g in range(N_PASS):
                cols = slice(g * PAIR + y * P, g * PAIR + (y + 1) * P)
                nc.tensor.matmul_mx(
                    out=t[:],
                    lhsT=wq[q][:, cols].bitcast(FP8X4),
                    lhsT_scale=ws[q][:, cols],
                    rhs=xq[g][:].bitcast(FP8X4),
                    rhs_scale=xs[g][:],
                    start=(g == 0),
                    stop=(g == N_PASS - 1),
                )

        us4 = {}

        def stt(q, y):
            if q < 0 or q >= N_PAIR:
                return
            col = (q // 8) * 16 + y * 8 + q % 8
            if y == 0:
                us4[q] = u_pool.tile([P, 4, S], F32, name="u4")
            outs = us4[q][:, 0:4:3, :] if y == 0 else us4[q][:, 1:3, :]
            table = tab0 if y == 0 else tab1
            n_cut = 2 if (q == N_PAIR - 1 and y == 1) else 1
            width = S // n_cut
            for c in range(n_cut):
                cols = slice(c * width, (c + 1) * width)
                nc.vector.scalar_tensor_tensor(
                    out=outs[:, :, cols],
                    in0=acc[(q, y)][:, cols].rearrange("p (o t) -> p o t", o=1).to_broadcast([P, 2, width]),
                    scalar=bcol[:, col:col + 1], in1=table[:, :, cols], op0=ALU.add, op1=ALU.mult,
                )

        def add(q):
            if q < 0 or q >= N_PAIR or q in T_ADD:
                return
            if port["last"] is not None:
                nc.gpsimd.tensor_copy(out=port["last"][0][:], in_=port["last"][1])
            nc.gpsimd.tensor_tensor(out=us4[q][:, 0:2, :], in0=us4[q][:, 0:2, :], in1=us4[q][:, 2:4, :], op=ALU.add)

        banks = {}
        ress = {}

        def ot(q, j):
            if q < 0 or q >= N_PAIR:
                return
            uc = us4[q]
            bank = tp_pool.tile([P, 2, 2, P], F32, name="bank")
            for a2 in range(2):
                cols = slice((2 * j + a2) * P, (2 * j + a2 + 1) * P)
                for y in range(2):
                    if q in T_ADD:
                        nc.tensor.matmul(out=bank[:, a2, y, :], lhsT=uc[:, y, cols], rhs=ident[:], is_transpose=True, start=True, stop=False)
                        nc.tensor.matmul(out=bank[:, a2, y, :], lhsT=uc[:, 2 + y, cols], rhs=ident[:], is_transpose=True, start=False, stop=True)
                    else:
                        nc.tensor.transpose(bank[:, a2, y, :], uc[:, y, cols], ident[:])
            if j == 0:
                ress[q] = res_pool.tile([P, 2, N_TOK, 2, HALF], F32, name="res")
            res = ress[q]
            copy_out = nc.vector.tensor_copy if (q, j) in V_OUT else nc.scalar.copy
            copy_out(
                out=res[:, :, 2 * j:2 * j + 2].rearrange("p x a y r -> p a y x r"),
                in_=bank[:].rearrange("p a y (x r) -> p a y x r", x=2),
            )
            dst = out_0 if q < 8 else out_1
            h0 = 2 * (q % 8)
            rows = dst[0, h0:h0 + 2].rearrange("x (p a) f -> p x a f", a=N_TOK)
            vals = res[:].rearrange("p x a y r -> p x a (y r)")
            if q in FINE_STORE:
                nc.sync.dma_start(out=rows[:, :, 2 * j:2 * j + 2, :], in_=vals[:, :, 2 * j:2 * j + 2, :])
            elif j == 1:
                nc.sync.dma_start(out=rows, in_=vals)

        ET = mybir.EngineType
        with tc.manual_schedule(engines={ET.PE, ET.DVE, ET.Pool, ET.Activation}):
            for g in range(N_PASS):
                xt(g)
                if g > 0:
                    xqz(g - 1)
            for s in range(2, N_DIRECT + RAW_BUFS):
                load_w(s)
            xqz(N_PASS - 1)
            bias_columns()
            back = {}
            for p in range(N_PAIR):
                back[p + LAG.get(p, 3)] = back.get(p + LAG.get(p, 3), []) + [p]
            for n in range(4):
                it(n // 2, n % 2)
                if n == 1:
                    table_sin()
                    table_cos()
                if n > 0:
                    qz((n - 1) // 2, (n - 1) % 2, (n - 1) % 2 + 1)
                if n == 2:
                    second_table()
            nxt = 4
            for q in range(0, N_PAIR + 2):
                due = back.get(q, [])
                if q > 0:
                    room = EARLY_HALVES.get(q, 3 - len(due))
                    for n in range(nxt, min(nxt + room, 2 * N_PAIR)):
                        it(n // 2, n % 2)
                    nxt = min(nxt + room, 2 * N_PAIR)
                if q == 0:
                    deint_s(2)
                elif q == 1:
                    deint_s(3)
                    deint_s(4)
                else:
                    deint_s(q + 3)
                for p in due:
                    ot(p, 0)
                    ot(p, 1)
                if q == 0:
                    deint_v(2)
                    qz(1, 1, 2)
                else:
                    qz(q + 1, 0, 2)
                    deint_v(q + 3)
                mx(q, 0)
                mx(q, 1)
                add(q - 1)
                stt(q, 0)
                stt(q, 1)
                if q == 0:
                    deint_v(3)
